import numpy as np
import ml_dtypes


def mxq(x, axis, fmt="e4m3"):
    dtype, down = {"e4m3": (ml_dtypes.float8_e4m3fn, 7), "e5m2": (ml_dtypes.float8_e5m2, 14)}[fmt]
    v = np.moveaxis(np.asarray(x, np.float32).astype(ml_dtypes.bfloat16).astype(np.float64), axis, -1)
    blocks = v.reshape(v.shape[:-1] + (-1, 32))
    amax = np.abs(blocks).max(-1, keepdims=True)
    byte = np.maximum(np.where(amax > 0, np.frexp(amax)[1] - 1 + 127, 0) - down, 1)
    scale = np.exp2(byte - 127.0)
    codes = (blocks / scale).astype(np.float32).astype(dtype).astype(np.float64)
    return np.moveaxis((codes * scale).reshape(v.shape), -1, axis)


BF16 = ml_dtypes.bfloat16


def bf(x):
    return np.asarray(x, np.float32).astype(BF16)


def f64(x):
    return np.asarray(x).astype(np.float64)


B, N, D, R = 4, 1024, 512, 4

TEMPERATURE = 1.0
EPS = 1e-12


def mix(a, c):
    return sum(a[:, :, r:r + 1] * c[:, r:r + 1, :] for r in range(R))


def setup_inputs():
    a = np.random.standard_normal((B, N, R))
    final = mix(a, np.random.standard_normal((B, R, D))) + 0.5 * np.random.standard_normal((B, N, D))
    mid = 0.5 * (mix(a, np.random.standard_normal((B, R, D))) + np.random.standard_normal((B, N, D)))
    return {"final_features": bf(final), "mid_features": bf(mid)}


def reference(final_features, mid_features):
    fin = f64(final_features)
    mid = f64(mid_features)
    norm = np.maximum(np.sqrt((mid ** 2).sum(-1, keepdims=True)), EPS)
    mq = mxq(mid / norm, 2, "e4m3")
    sim = mq @ mq.transpose(0, 2, 1)
    sim = sim * (1.0 - np.eye(N))[None, :, :]
    confidence = sim.max(-1)
    z = sim / TEMPERATURE
    e = np.exp(z - z.max(-1, keepdims=True))
    refined = (mxq(e, 2, "e4m3") @ mxq(fin, 1, "e4m3")) / e.sum(-1, keepdims=True)
    cw = confidence[..., None]
    return cw * refined + (1.0 - cw) * fin

@@ -1,0 +1,300 @@
+from contextlib import ExitStack
+
+import concourse.mybir as mybir
+from concourse.masks import make_identity
+
+BF16 = mybir.dt.bfloat16
+F32 = mybir.dt.float32
+U32 = mybir.dt.uint32
+U8 = mybir.dt.uint8
+FP8X4 = mybir.dt.float8_e4m3fn_x4
+ALU = mybir.AluOpType
+FUNC = mybir.ActivationFunctionType
+AXIS = mybir.AxisListType
+
+B = 4
+N = 1024
+D = 512
+P = 128
+PACK = 4
+K_PASS = P * PACK
+TILES = N // P
+G = N // K_PASS
+BANK = 512
+HALF = PACK
+ROWS = B * TILES
+EPS = 1e-12
+
+MID_AHEAD = 13
+FIN_AHEAD = 5
+PV_BEHIND = 4
+
+FLOPS = 2 * B * N * N * D * 2
+
+
+def tile_similarityenhancementmodule_t_kernel(tc, final_features, mid_features, out):
+    nc = tc.nc
+    with ExitStack() as stack:
+        stack.enter_context(tc.manual_schedule())
+        const = stack.enter_context(tc.tile_pool(name="const", bufs=1))
+        loads = stack.enter_context(tc.tile_pool(name="loads", bufs=B))
+        codes = stack.enter_context(tc.tile_pool(name="codes", bufs=2))
+        ring = stack.enter_context(tc.tile_pool(name="ring", bufs=3))
+        small = stack.enter_context(tc.tile_pool(name="small", bufs=4))
+        late = stack.enter_context(tc.tile_pool(name="late", bufs=2 * PV_BEHIND))
+        psum2 = stack.enter_context(tc.psum_pool(name="psum2", bufs=2))
+        psum1 = stack.enter_context(tc.psum_pool(name="psum1", bufs=1))
+
+        def token_view(dram_batch):
+            return dram_batch.rearrange("(g p t) d -> p g t d", g=G, p=P, t=PACK)
+
+        mid_sb = []
+        fin_sb = []
+
+        def load_mid(b):
+            mid_t = loads.tile([P, G, PACK, D], BF16, name="mid_t")
+            for g in range(G):
+                nc.sync.dma_start(out=mid_t[:, g, :, :], in_=token_view(mid_features[b])[:, g, :, :])
+            mid_sb.append(mid_t)
+
+        def load_fin(b):
+            fin_t = loads.tile([P, G, PACK, D], BF16, name="fin_t")
+            nc.sync.dma_start(out=fin_t[:], in_=token_view(final_features[b]))
+            fin_sb.append(fin_t)
+
+        load_mid(0)
+        for b in range(B):
+            if b + 1 < B:
+                load_mid(b + 1)
+            load_fin(b)
+
+        ident = const.tile([P, P], BF16)
+        make_identity(nc, ident[:])
+        ident_f = const.tile([P, P], F32)
+        make_identity(nc, ident_f[:])
+        off_diag = const.tile([P, P], F32)
+        nc.vector.tensor_scalar(
+            out=off_diag[:], in0=ident_f[:], scalar1=-1.0, scalar2=1.0, op0=ALU.mult, op1=ALU.add
+        )
+        neg_half = const.tile([P, 1], F32)
+        nc.vector.memset(neg_half[:], -0.5)
+
+        sumsq, inv_norm, mid_n, mid_tr, mid_grouped = {}, {}, {}, {}, {}
+        mid_codes, mid_scales, fin_codes, fin_scales, fin_grouped = {}, {}, {}, {}, {}
+        sim, head, neg_c, sums, e_row, e_tr, e_grouped, e_codes, e_scales = {}, {}, {}, {}, {}, {}, {}, {}, {}
+        gain, keep, acc, kept, blended = {}, {}, {}, {}, {}
+
+        def square(u):
+            b, a = divmod(u, TILES)
+            g, t = divmod(a, PACK)
+            squares = ring.tile([P, D], BF16)
+            total = small.tile([P, 1], F32, name="total")
+            nc.scalar.activation(out=squares[:], in_=mid_sb[b][:, g, t, :], func=FUNC.Square, accum_out=total[:])
+            sumsq[u] = total
+
+        def norm(u):
+            clamped = small.tile([P, 1], F32)
+            nc.gpsimd.tensor_scalar_max(out=clamped[:], in0=sumsq[u][:], scalar1=EPS * EPS)
+            inverse = small.tile([P, 1], F32)
+            nc.gpsimd.tensor_tensor(out=inverse[:], in0=clamped[:], in1=neg_half[:], op=ALU.pow)
+            inv_norm[u] = inverse
+
+        def scale(u):
+            b, a = divmod(u, TILES)
+            g, t = divmod(a, PACK)
+            normed = ring.tile([P, D], BF16)
+            nc.vector.tensor_scalar_mul(out=normed[:], in0=mid_sb[b][:, g, t, :], scalar1=inv_norm[u][:])
+            mid_n[u] = normed
+
+        def tr_mid(u):
+            turned = psum1.tile([P, PACK, P], BF16, name="mid_turned")
+            for c in range(PACK):
+                nc.tensor.transpose(turned[:, c, :], mid_n[u][:, P * c : P * (c + 1)], ident[:])
+            mid_tr[u] = turned
+
+        def copy_mid(u):
+            grouped = ring.tile([P, P, PACK], BF16, name="mid_g", align_bytes=64)
+            if u % 2 == 0:
+                nc.vector.tensor_copy(out=grouped[:], in_=mid_tr[u][:].rearrange("p c w -> p w c"))
+            else:
+                nc.scalar.copy(out=grouped[:], in_=mid_tr[u][:].rearrange("p c w -> p w c"))
+            mid_grouped[u] = grouped
+
+        def quant_mid(u):
+            b, a = divmod(u, TILES)
+            if a == 0:
+                words = codes.tile([P, N], U32, name="mid_words", align_bytes=64)
+                plane = codes.tile([P, N], U8, name="mid_plane", align_bytes=64)
+                mid_codes[b], mid_scales[b] = words, plane
+            nc.vector.quantize_mx(
+                out=mid_codes[b][:, P * a : P * (a + 1)].bitcast(FP8X4),
+                scales=mid_scales[b][:, P * a : P * (a + 1)],
+                in_=mid_grouped[u][:].rearrange("p w c -> p (w c)"),
+            )
+
+        def regroup_fin(u):
+            b, r = divmod(u, TILES)
+            g, q = divmod(r, PACK)
+            grouped = ring.tile([P, P, PACK], BF16, name="fin_g", align_bytes=64)
+            nc.vector.tensor_copy(
+                out=grouped[:].rearrange("p (c i) t -> p c t i", i=4),
+                in_=fin_sb[b][:, g, :, P * q : P * (q + 1)].rearrange("p t (c i) -> p c t i", i=4),
+            )
+            fin_grouped[u] = grouped
+
+        def quant_fin(u):
+            b, r = divmod(u, TILES)
+            g, q = divmod(r, PACK)
+            if r == 0:
+                words = codes.tile([P, G, D], U32, name="fin_words", align_bytes=64)
+                plane = codes.tile([P, G, D], U8, name="fin_plane", align_bytes=64)
+                fin_codes[b], fin_scales[b] = words, plane
+            nc.vector.quantize_mx(
+                out=fin_codes[b][:, g, P * q : P * (q + 1)].bitcast(FP8X4),
+                scales=fin_scales[b][:, g, P * q : P * (q + 1)],
+                in_=fin_grouped[u][:].rearrange("p d t -> p (d t)"),
+            )
+
+        def sim_rows(s):
+            b, a = divmod(s, TILES)
+            banks = [psum2.tile([P, BANK], F32, name="sim%d" % h) for h in range(2)]
+            for nb in range(TILES):
+                kb = (a + nb) % TILES
+                h, q = divmod(nb, PACK)
+                nc.tensor.matmul_mx(
+                    out=banks[h][:, P * q : P * (q + 1)],
+                    lhsT=mid_codes[b][:, P * a : P * (a + 1)].bitcast(FP8X4),
+                    lhsT_scale=mid_scales[b][:, P * a : P * (a + 1)],
+                    rhs=mid_codes[b][:, P * kb : P * (kb + 1)].bitcast(FP8X4),
+                    rhs_scale=mid_scales[b][:, P * kb : P * (kb + 1)],
+                    start=True,
+                    stop=True,
+                )
+            sim[s] = banks
+
+        def mask_max(s):
+            h, j = divmod(s, HALF)
+            if j == 0:
+                minus_c = small.tile([P, HALF], F32, name="minus_c")
+                parts = small.tile([P, HALF, 3], F32, name="parts")
+                neg_c[h], sums[h] = minus_c, parts
+            first = ring.tile([P, P + 2], F32, name="first")
+            nc.vector.tensor_tensor(out=first[:, 0:P], in0=sim[s][0][:, 0:P], in1=off_diag[:], op=ALU.mult)
+            nc.vector.tensor_reduce(out=first[:, P : P + 1], in_=sim[s][0][:, P:BANK], axis=AXIS.X, op=ALU.max)
+            nc.vector.tensor_reduce(out=first[:, P + 1 : P + 2], in_=sim[s][1][:], axis=AXIS.X, op=ALU.max)
+            nc.vector.tensor_reduce(out=neg_c[h][:, j : j + 1], in_=first[:], axis=AXIS.X, op=ALU.max, negate=True)
+            head[s] = first
+
+        def exp_rows(s):
+            h, j = divmod(s, HALF)
+            e = ring.tile([P, N], BF16, name="e")
+            bias = neg_c[h][:, j : j + 1]
+            nc.scalar.activation(
+                out=e[:, 0:P], in_=head[s][:, 0:P], func=FUNC.Exp, bias=bias, accum_out=sums[h][:, j, 0:1]
+            )
+            nc.scalar.activation(
+                out=e[:, P:BANK], in_=sim[s][0][:, P:BANK], func=FUNC.Exp, bias=bias, accum_out=sums[h][:, j, 1:2]
+            )
+            nc.scalar.activation(
+                out=e[:, BANK:N], in_=sim[s][1][:], func=FUNC.Exp, bias=bias, accum_out=sums[h][:, j, 2:3]
+            )
+            e_row[s] = e
+
+        def tr_e(s):
+            a = s % TILES
+            turned = psum1.tile([P, TILES, P], BF16, name="e_turned")
+            for nb in range(TILES):
+                kb = (a + nb) % TILES
+                nc.tensor.transpose(turned[:, kb, :], e_row[s][:, P * nb : P * (nb + 1)], ident[:])
+            e_tr[s] = turned
+
+        def copy_e(s):
+            grouped = ring.tile([P, G, P, PACK], BF16, name="e_g", align_bytes=64)
+            nc.scalar.copy(out=grouped[:], in_=e_tr[s][:].rearrange("p (g t) w -> p g w t", g=G))
+            e_grouped[s] = grouped
+
+        def quant_e(s):
+            words = late.tile([P, G * P], U32, name="e_words", align_bytes=64)
+            plane = late.tile([P, G * P], U8, name="e_plane", align_bytes=64)
+            nc.vector.quantize_mx(
+                out=words[:].bitcast(FP8X4), scales=plane[:], in_=e_grouped[s][:].rearrange("p g w t -> p (g w t)")
+            )
+            e_codes[s], e_scales[s] = words, plane
+
+        def factors(h):
+            row_sum = small.tile([P, HALF], F32)
+            nc.vector.tensor_reduce(out=row_sum[:], in_=sums[h][:], axis=AXIS.X, op=ALU.add)
+            inv_sum = small.tile([P, HALF], F32)
+            nc.vector.reciprocal(out=inv_sum[:], in_=row_sum[:])
+            c_over_sum = small.tile([P, HALF], F32)
+            nc.vector.scalar_tensor_tensor(
+                out=c_over_sum[:], in0=neg_c[h][:], scalar=-1.0, in1=inv_sum[:], op0=ALU.mult, op1=ALU.mult
+            )
+            one_minus_c = small.tile([P, HALF], F32)
+            nc.vector.tensor_scalar_add(out=one_minus_c[:], in0=neg_c[h][:], scalar1=1.0)
+            gain[h], keep[h] = c_over_sum, one_minus_c
+
+        def pv(s):
+            b = s // TILES
+            total = psum2.tile([P, D], F32, name="pv_total")
+            for g in range(G):
+                nc.tensor.matmul_mx(
+                    out=total[:],
+                    lhsT=e_codes[s][:, P * g : P * (g + 1)].bitcast(FP8X4),
+                    lhsT_scale=e_scales[s][:, P * g : P * (g + 1)],
+                    rhs=fin_codes[b][:, g, :].bitcast(FP8X4),
+                    rhs_scale=fin_scales[b][:, g, :],
+                    start=(g == 0),
+                    stop=(g == G - 1),
+                )
+            acc[s] = total
+
+        def keep_fin(s):
+            b, a = divmod(s, TILES)
+            g, t = divmod(a, PACK)
+            h, j = divmod(s, HALF)
+            part = ring.tile([P, D], F32, name="part")
+            nc.gpsimd.tensor_scalar(
+                out=part[:], in0=fin_sb[b][:, g, t, :], scalar1=keep[h][:, j : j + 1], scalar2=0.0,
+                op0=ALU.mult, op1=ALU.add,
+            )
+            kept[s] = part
+
+        def blend(s):
+            b, a = divmod(s, TILES)
+            g, t = divmod(a, PACK)
+            h, j = divmod(s, HALF)
+            if s % 2 == 0:
+                pair = ring.tile([P, 2, D], F32, name="pair")
+                blended[s // 2] = pair
+            nc.vector.scalar_tensor_tensor(
+                out=blended[s // 2][:, s % 2, :], in0=acc[s][:], scalar=gain[h][:, j : j + 1], in1=kept[s][:],
+                op0=ALU.mult, op1=ALU.add,
+            )
+            if s % 2 == 1:
+                nc.sync.dma_start(out=token_view(out[b])[:, g, t - 1 : t + 1, :], in_=blended[s // 2][:])
+
+        def run(stage, index, count):
+            if 0 <= index < count:
+                stage(index)
+
+        for i in range(-MID_AHEAD, ROWS + PV_BEHIND + 2):
+            run(tr_e, i - 1, ROWS)
+            run(mask_max, i + 1, ROWS)
+            run(exp_rows, i, ROWS)
+            run(sim_rows, i + 2, ROWS)
+            run(copy_e, i - 1, ROWS)
+            run(pv, i - PV_BEHIND, ROWS)
+            run(blend, i - PV_BEHIND - 1, ROWS)
+            run(scale, i + MID_AHEAD - 1, ROWS)
+            run(copy_mid, i + MID_AHEAD - 2, ROWS)
+            run(tr_mid, i + MID_AHEAD - 1, ROWS)
+            run(square, i + MID_AHEAD, ROWS)
+            run(norm, i + MID_AHEAD, ROWS)
+            run(quant_mid, i + MID_AHEAD - 3, ROWS)
+            run(regroup_fin, i + FIN_AHEAD, ROWS)
+            run(quant_fin, i + FIN_AHEAD - 1, ROWS)
+            run(quant_e, i - 2, ROWS)
+            if i % HALF == HALF - 1:
+                run(factors, i // HALF, ROWS // HALF)
+            run(keep_fin, i - PV_BEHIND, ROWS)

@@ -25,7 +25,7 @@ HALF = PACK
 ROWS = B * TILES
 EPS = 1e-12
 
-MID_AHEAD = 13
+MID_AHEAD = 15
 FIN_AHEAD = 5
 PV_BEHIND = 4
 
@@ -42,8 +42,7 @@ def tile_similarityenhancementmodule_t_kernel(tc, final_features, mid_features, 
         ring = stack.enter_context(tc.tile_pool(name="ring", bufs=3))
         small = stack.enter_context(tc.tile_pool(name="small", bufs=4))
         late = stack.enter_context(tc.tile_pool(name="late", bufs=2 * PV_BEHIND))
-        psum2 = stack.enter_context(tc.psum_pool(name="psum2", bufs=2))
-        psum1 = stack.enter_context(tc.psum_pool(name="psum1", bufs=1))
+        psum = stack.enter_context(tc.psum_pool(name="psum", bufs=2))
 
         def token_view(dram_batch):
             return dram_batch.rearrange("(g p t) d -> p g t d", g=G, p=P, t=PACK)
@@ -82,7 +81,7 @@ def tile_similarityenhancementmodule_t_kernel(tc, final_features, mid_features, 
         sumsq, inv_norm, mid_n, mid_tr, mid_grouped = {}, {}, {}, {}, {}
         mid_codes, mid_scales, fin_codes, fin_scales, fin_grouped = {}, {}, {}, {}, {}
         sim, head, neg_c, sums, e_row, e_tr, e_grouped, e_codes, e_scales = {}, {}, {}, {}, {}, {}, {}, {}, {}
-        gain, keep, acc, kept, blended = {}, {}, {}, {}, {}
+        gain, acc, kept, blended = {}, {}, {}, {}
 
         def square(u):
             b, a = divmod(u, TILES)
@@ -107,7 +106,7 @@ def tile_similarityenhancementmodule_t_kernel(tc, final_features, mid_features, 
             mid_n[u] = normed
 
         def tr_mid(u):
-            turned = psum1.tile([P, PACK, P], BF16, name="mid_turned")
+            turned = psum.tile([P, PACK, P], BF16, name="mid_turned", tag="turned")
             for c in range(PACK):
                 nc.tensor.transpose(turned[:, c, :], mid_n[u][:, P * c : P * (c + 1)], ident[:])
             mid_tr[u] = turned
@@ -157,7 +156,7 @@ def tile_similarityenhancementmodule_t_kernel(tc, final_features, mid_features, 
 
         def sim_rows(s):
             b, a = divmod(s, TILES)
-            banks = [psum2.tile([P, BANK], F32, name="sim%d" % h) for h in range(2)]
+            banks = [psum.tile([P, BANK], F32, name="sim%d" % h) for h in range(2)]
             for nb in range(TILES):
                 kb = (a + nb) % TILES
                 h, q = divmod(nb, PACK)
@@ -202,7 +201,7 @@ def tile_similarityenhancementmodule_t_kernel(tc, final_features, mid_features, 
 
         def tr_e(s):
             a = s % TILES
-            turned = psum1.tile([P, TILES, P], BF16, name="e_turned")
+            turned = psum.tile([P, TILES, P], BF16, name="e_turned", tag="turned")
             for nb in range(TILES):
                 kb = (a + nb) % TILES
                 nc.tensor.transpose(turned[:, kb, :], e_row[s][:, P * nb : P * (nb + 1)], ident[:])
@@ -230,13 +229,11 @@ def tile_similarityenhancementmodule_t_kernel(tc, final_features, mid_features, 
             nc.vector.scalar_tensor_tensor(
                 out=c_over_sum[:], in0=neg_c[h][:], scalar=-1.0, in1=inv_sum[:], op0=ALU.mult, op1=ALU.mult
             )
-            one_minus_c = small.tile([P, HALF], F32)
-            nc.vector.tensor_scalar_add(out=one_minus_c[:], in0=neg_c[h][:], scalar1=1.0)
-            gain[h], keep[h] = c_over_sum, one_minus_c
+            gain[h] = c_over_sum
 
         def pv(s):
             b = s // TILES
-            total = psum2.tile([P, D], F32, name="pv_total")
+            total = psum.tile([P, D], F32, name="pv_total")
             for g in range(G):
                 nc.tensor.matmul_mx(
                     out=total[:],
@@ -253,9 +250,11 @@ def tile_similarityenhancementmodule_t_kernel(tc, final_features, mid_features, 
             b, a = divmod(s, TILES)
             g, t = divmod(a, PACK)
             h, j = divmod(s, HALF)
-            part = ring.tile([P, D], F32, name="part")
+            one_minus_c = small.tile([P, 1], F32)
+            nc.gpsimd.tensor_scalar_add(out=one_minus_c[:], in0=neg_c[h][:, j : j + 1], scalar1=1.0)
+            part = late.tile([P, D], F32, name="part")
             nc.gpsimd.tensor_scalar(
-                out=part[:], in0=fin_sb[b][:, g, t, :], scalar1=keep[h][:, j : j + 1], scalar2=0.0,
+                out=part[:], in0=fin_sb[b][:, g, t, :], scalar1=one_minus_c[:], scalar2=0.0,
                 op0=ALU.mult, op1=ALU.add,
             )
             kept[s] = part
@@ -280,21 +279,21 @@ def tile_similarityenhancementmodule_t_kernel(tc, final_features, mid_features, 
 
         for i in range(-MID_AHEAD, ROWS + PV_BEHIND + 2):
             run(tr_e, i - 1, ROWS)
+            run(copy_mid, i + MID_AHEAD - 4, ROWS)
+            run(tr_mid, i + MID_AHEAD - 3, ROWS)
             run(mask_max, i + 1, ROWS)
             run(exp_rows, i, ROWS)
             run(sim_rows, i + 2, ROWS)
             run(copy_e, i - 1, ROWS)
             run(pv, i - PV_BEHIND, ROWS)
+            run(keep_fin, i, ROWS)
             run(blend, i - PV_BEHIND - 1, ROWS)
-            run(scale, i + MID_AHEAD - 1, ROWS)
-            run(copy_mid, i + MID_AHEAD - 2, ROWS)
-            run(tr_mid, i + MID_AHEAD - 1, ROWS)
+            run(scale, i + MID_AHEAD - 2, ROWS)
             run(square, i + MID_AHEAD, ROWS)
             run(norm, i + MID_AHEAD, ROWS)
-            run(quant_mid, i + MID_AHEAD - 3, ROWS)
+            run(quant_mid, i + MID_AHEAD - 5, ROWS)
             run(regroup_fin, i + FIN_AHEAD, ROWS)
             run(quant_fin, i + FIN_AHEAD - 1, ROWS)
             run(quant_e, i - 2, ROWS)
             if i % HALF == HALF - 1:
                 run(factors, i // HALF, ROWS // HALF)
-            run(keep_fin, i - PV_BEHIND, ROWS)

@@ -77,6 +77,8 @@ def tile_similarityenhancementmodule_t_kernel(tc, final_features, mid_features, 
         )
         neg_half = const.tile([P, 1], F32)
         nc.vector.memset(neg_half[:], -0.5)
+        neg_one = const.tile([P, HALF], F32)
+        nc.vector.memset(neg_one[:], -1.0)
 
         sumsq, inv_norm, mid_n, mid_tr, mid_grouped = {}, {}, {}, {}, {}
         mid_codes, mid_scales, fin_codes, fin_scales, fin_grouped = {}, {}, {}, {}, {}
@@ -181,8 +183,11 @@ def tile_similarityenhancementmodule_t_kernel(tc, final_features, mid_features, 
             nc.vector.tensor_tensor(out=first[:, 0:P], in0=sim[s][0][:, 0:P], in1=off_diag[:], op=ALU.mult)
             nc.vector.tensor_reduce(out=first[:, P : P + 1], in_=sim[s][0][:, P:BANK], axis=AXIS.X, op=ALU.max)
             nc.vector.tensor_reduce(out=first[:, P + 1 : P + 2], in_=sim[s][1][:], axis=AXIS.X, op=ALU.max)
-            nc.vector.tensor_reduce(out=neg_c[h][:, j : j + 1], in_=first[:], axis=AXIS.X, op=ALU.max, negate=True)
             head[s] = first
+
+        def row_max(s):
+            h, j = divmod(s, HALF)
+            nc.vector.tensor_reduce(out=neg_c[h][:, j : j + 1], in_=head[s][:], axis=AXIS.X, op=ALU.max, negate=True)
 
         def exp_rows(s):
             h, j = divmod(s, HALF)
@@ -221,14 +226,16 @@ def tile_similarityenhancementmodule_t_kernel(tc, final_features, mid_features, 
             e_codes[s], e_scales[s] = words, plane
 
         def factors(h):
+            two = small.tile([P, HALF], F32)
+            nc.gpsimd.tensor_tensor(out=two[:], in0=sums[h][:, :, 0], in1=sums[h][:, :, 1], op=ALU.add)
             row_sum = small.tile([P, HALF], F32)
-            nc.vector.tensor_reduce(out=row_sum[:], in_=sums[h][:], axis=AXIS.X, op=ALU.add)
+            nc.gpsimd.tensor_tensor(out=row_sum[:], in0=two[:], in1=sums[h][:, :, 2], op=ALU.add)
             inv_sum = small.tile([P, HALF], F32)
-            nc.vector.reciprocal(out=inv_sum[:], in_=row_sum[:])
+            nc.gpsimd.tensor_tensor(out=inv_sum[:], in0=row_sum[:], in1=neg_one[:], op=ALU.pow)
+            c = small.tile([P, HALF], F32)
+            nc.gpsimd.tensor_scalar(out=c[:], in0=neg_c[h][:], scalar1=-1.0, scalar2=0.0, op0=ALU.mult, op1=ALU.add)
             c_over_sum = small.tile([P, HALF], F32)
-            nc.vector.scalar_tensor_tensor(
-                out=c_over_sum[:], in0=neg_c[h][:], scalar=-1.0, in1=inv_sum[:], op0=ALU.mult, op1=ALU.mult
-            )
+            nc.gpsimd.tensor_tensor(out=c_over_sum[:], in0=c[:], in1=inv_sum[:], op=ALU.mult)
             gain[h] = c_over_sum
 
         def pv(s):
@@ -288,6 +295,7 @@ def tile_similarityenhancementmodule_t_kernel(tc, final_features, mid_features, 
             run(pv, i - PV_BEHIND, ROWS)
             run(keep_fin, i, ROWS)
             run(blend, i - PV_BEHIND - 1, ROWS)
+            run(row_max, i + 1, ROWS)
             run(scale, i + MID_AHEAD - 2, ROWS)
             run(square, i + MID_AHEAD, ROWS)
             run(norm, i + MID_AHEAD, ROWS)

@@ -25,7 +25,7 @@ HALF = PACK
 ROWS = B * TILES
 EPS = 1e-12
 
-MID_AHEAD = 15
+MID_AHEAD = 16
 FIN_AHEAD = 5
 PV_BEHIND = 4
 
@@ -77,13 +77,11 @@ def tile_similarityenhancementmodule_t_kernel(tc, final_features, mid_features, 
         )
         neg_half = const.tile([P, 1], F32)
         nc.vector.memset(neg_half[:], -0.5)
-        neg_one = const.tile([P, HALF], F32)
-        nc.vector.memset(neg_one[:], -1.0)
 
         sumsq, inv_norm, mid_n, mid_tr, mid_grouped = {}, {}, {}, {}, {}
         mid_codes, mid_scales, fin_codes, fin_scales, fin_grouped = {}, {}, {}, {}, {}
         sim, head, neg_c, sums, e_row, e_tr, e_grouped, e_codes, e_scales = {}, {}, {}, {}, {}, {}, {}, {}, {}
-        gain, acc, kept, blended = {}, {}, {}, {}
+        row_sum, inv_sum, gain, keep, acc, kept, blended = {}, {}, {}, {}, {}, {}, {}
 
         def square(u):
             b, a = divmod(u, TILES)
@@ -225,18 +223,28 @@ def tile_similarityenhancementmodule_t_kernel(tc, final_features, mid_features, 
             )
             e_codes[s], e_scales[s] = words, plane
 
-        def factors(h):
-            two = small.tile([P, HALF], F32)
-            nc.gpsimd.tensor_tensor(out=two[:], in0=sums[h][:, :, 0], in1=sums[h][:, :, 1], op=ALU.add)
-            row_sum = small.tile([P, HALF], F32)
-            nc.gpsimd.tensor_tensor(out=row_sum[:], in0=two[:], in1=sums[h][:, :, 2], op=ALU.add)
-            inv_sum = small.tile([P, HALF], F32)
-            nc.gpsimd.tensor_tensor(out=inv_sum[:], in0=row_sum[:], in1=neg_one[:], op=ALU.pow)
-            c = small.tile([P, HALF], F32)
-            nc.gpsimd.tensor_scalar(out=c[:], in0=neg_c[h][:], scalar1=-1.0, scalar2=0.0, op0=ALU.mult, op1=ALU.add)
+        def add_sums(h):
+            total = small.tile([P, HALF], F32, name="row_total")
+            nc.vector.tensor_reduce(out=total[:], in_=sums[h][:], axis=AXIS.X, op=ALU.add)
+            row_sum[h] = total
+
+        def invert_sums(h):
+            inverse = small.tile([P, HALF], F32, name="row_inverse")
+            nc.vector.reciprocal(out=inverse[:], in_=row_sum[h][:])
+            inv_sum[h] = inverse
+
+        def gains(h):
             c_over_sum = small.tile([P, HALF], F32)
-            nc.gpsimd.tensor_tensor(out=c_over_sum[:], in0=c[:], in1=inv_sum[:], op=ALU.mult)
+            nc.vector.scalar_tensor_tensor(
+                out=c_over_sum[:], in0=neg_c[h][:], scalar=-1.0, in1=inv_sum[h][:], op0=ALU.mult, op1=ALU.mult
+            )
             gain[h] = c_over_sum
+
+        def keep_factor(s):
+            h, j = divmod(s, HALF)
+            one_minus_c = small.tile([P, 1], F32)
+            nc.vector.tensor_scalar_add(out=one_minus_c[:], in0=neg_c[h][:, j : j + 1], scalar1=1.0)
+            keep[s] = one_minus_c
 
         def pv(s):
             b = s // TILES
@@ -257,11 +265,9 @@ def tile_similarityenhancementmodule_t_kernel(tc, final_features, mid_features, 
             b, a = divmod(s, TILES)
             g, t = divmod(a, PACK)
             h, j = divmod(s, HALF)
-            one_minus_c = small.tile([P, 1], F32)
-            nc.gpsimd.tensor_scalar_add(out=one_minus_c[:], in0=neg_c[h][:, j : j + 1], scalar1=1.0)
             part = late.tile([P, D], F32, name="part")
             nc.gpsimd.tensor_scalar(
-                out=part[:], in0=fin_sb[b][:, g, t, :], scalar1=one_minus_c[:], scalar2=0.0,
+                out=part[:], in0=fin_sb[b][:, g, t, :], scalar1=keep[s][:], scalar2=0.0,
                 op0=ALU.mult, op1=ALU.add,
             )
             kept[s] = part
@@ -285,23 +291,26 @@ def tile_similarityenhancementmodule_t_kernel(tc, final_features, mid_features, 
                 stage(index)
 
         for i in range(-MID_AHEAD, ROWS + PV_BEHIND + 2):
+            done_half = i // HALF - 1 if i % HALF == 0 else -1
             run(tr_e, i - 1, ROWS)
-            run(copy_mid, i + MID_AHEAD - 4, ROWS)
-            run(tr_mid, i + MID_AHEAD - 3, ROWS)
+            run(copy_mid, i + MID_AHEAD - 5, ROWS)
+            run(tr_mid, i + MID_AHEAD - 4, ROWS)
             run(mask_max, i + 1, ROWS)
+            run(add_sums, done_half, ROWS // HALF)
             run(exp_rows, i, ROWS)
             run(sim_rows, i + 2, ROWS)
             run(copy_e, i - 1, ROWS)
             run(pv, i - PV_BEHIND, ROWS)
-            run(keep_fin, i, ROWS)
             run(blend, i - PV_BEHIND - 1, ROWS)
+            run(invert_sums, done_half, ROWS // HALF)
             run(row_max, i + 1, ROWS)
-            run(scale, i + MID_AHEAD - 2, ROWS)
+            run(gains, done_half, ROWS // HALF)
             run(square, i + MID_AHEAD, ROWS)
-            run(norm, i + MID_AHEAD, ROWS)
-            run(quant_mid, i + MID_AHEAD - 5, ROWS)
+            run(scale, i + MID_AHEAD - 3, ROWS)
+            run(quant_mid, i + MID_AHEAD - 6, ROWS)
             run(regroup_fin, i + FIN_AHEAD, ROWS)
             run(quant_fin, i + FIN_AHEAD - 1, ROWS)
             run(quant_e, i - 2, ROWS)
-            if i % HALF == HALF - 1:
-                run(factors, i // HALF, ROWS // HALF)
+            run(keep_factor, i + 1, ROWS)
+            run(keep_fin, i + 1, ROWS)
+            run(norm, i + MID_AHEAD - 1, ROWS)

@@ -25,9 +25,10 @@ HALF = PACK
 ROWS = B * TILES
 EPS = 1e-12
 
-MID_AHEAD = 16
-FIN_AHEAD = 5
-PV_BEHIND = 4
+MID_AHEAD = 13
+FIN_AHEAD = 6
+PV_BEHIND = 3
+FIRST = -3
 
 FLOPS = 2 * B * N * N * D * 2
 
@@ -38,8 +39,8 @@ def tile_similarityenhancementmodule_t_kernel(tc, final_features, mid_features, 
         stack.enter_context(tc.manual_schedule())
         const = stack.enter_context(tc.tile_pool(name="const", bufs=1))
         loads = stack.enter_context(tc.tile_pool(name="loads", bufs=B))
-        codes = stack.enter_context(tc.tile_pool(name="codes", bufs=2))
-        ring = stack.enter_context(tc.tile_pool(name="ring", bufs=3))
+        codes = stack.enter_context(tc.tile_pool(name="codes", bufs=3))
+        ring = stack.enter_context(tc.tile_pool(name="ring", bufs=4))
         small = stack.enter_context(tc.tile_pool(name="small", bufs=4))
         late = stack.enter_context(tc.tile_pool(name="late", bufs=2 * PV_BEHIND))
         psum = stack.enter_context(tc.psum_pool(name="psum", bufs=2))
@@ -53,7 +54,9 @@ def tile_similarityenhancementmodule_t_kernel(tc, final_features, mid_features, 
         def load_mid(b):
             mid_t = loads.tile([P, G, PACK, D], BF16, name="mid_t")
             for g in range(G):
-                nc.sync.dma_start(out=mid_t[:, g, :, :], in_=token_view(mid_features[b])[:, g, :, :])
+                for t in range(0, PACK, 2 if b == 0 and g == 0 else PACK):
+                    last = t + 2 if b == 0 and g == 0 else PACK
+                    nc.sync.dma_start(out=mid_t[:, g, t:last, :], in_=token_view(mid_features[b])[:, g, t:last, :])
             mid_sb.append(mid_t)
 
         def load_fin(b):
@@ -75,7 +78,7 @@ def tile_similarityenhancementmodule_t_kernel(tc, final_features, mid_features, 
         nc.vector.tensor_scalar(
             out=off_diag[:], in0=ident_f[:], scalar1=-1.0, scalar2=1.0, op0=ALU.mult, op1=ALU.add
         )
-        neg_half = const.tile([P, 1], F32)
+        neg_half = const.tile([P, PACK], F32)
         nc.vector.memset(neg_half[:], -0.5)
 
         sumsq, inv_norm, mid_n, mid_tr, mid_grouped = {}, {}, {}, {}, {}
@@ -83,37 +86,54 @@ def tile_similarityenhancementmodule_t_kernel(tc, final_features, mid_features, 
         sim, head, neg_c, sums, e_row, e_tr, e_grouped, e_codes, e_scales = {}, {}, {}, {}, {}, {}, {}, {}, {}
         row_sum, inv_sum, gain, keep, acc, kept, blended = {}, {}, {}, {}, {}, {}, {}
 
-        def square(u):
+        def group_of(u):
+            size = PACK if u < TILES else 2
+            return u - u % size, size
+
+        def square(u, on_scalar):
             b, a = divmod(u, TILES)
             g, t = divmod(a, PACK)
-            squares = ring.tile([P, D], BF16)
-            total = small.tile([P, 1], F32, name="total")
-            nc.scalar.activation(out=squares[:], in_=mid_sb[b][:, g, t, :], func=FUNC.Square, accum_out=total[:])
-            sumsq[u] = total
+            first, size = group_of(u)
+            if first not in sumsq:
+                total = small.tile([P, PACK], F32, name="total")
+                sumsq[first] = total
+            squares = ring.tile([P, D], BF16, name="squares")
+            one = mid_sb[b][:, g, t, :]
+            to = sumsq[first][:, u - first : u - first + 1]
+            if on_scalar:
+                nc.scalar.activation(out=squares[:], in_=one, func=FUNC.Square, accum_out=to)
+            else:
+                nc.vector.scalar_tensor_tensor(
+                    out=squares[:], in0=one, scalar=1.0, in1=one, op0=ALU.mult, op1=ALU.mult, accum_out=to
+                )
 
         def norm(u):
-            clamped = small.tile([P, 1], F32)
-            nc.gpsimd.tensor_scalar_max(out=clamped[:], in0=sumsq[u][:], scalar1=EPS * EPS)
-            inverse = small.tile([P, 1], F32)
-            nc.gpsimd.tensor_tensor(out=inverse[:], in0=clamped[:], in1=neg_half[:], op=ALU.pow)
-            inv_norm[u] = inverse
+            first, size = group_of(u)
+            clamped = small.tile([P, PACK], F32, name="clamped")
+            nc.gpsimd.tensor_scalar_max(out=clamped[:, 0:size], in0=sumsq[first][:, 0:size], scalar1=EPS * EPS)
+            inverse = small.tile([P, PACK], F32, name="inverse")
+            nc.gpsimd.tensor_tensor(
+                out=inverse[:, 0:size], in0=clamped[:, 0:size], in1=neg_half[:, 0:size], op=ALU.pow
+            )
+            for j in range(size):
+                inv_norm[first + j] = inverse[:, j : j + 1]
 
         def scale(u):
             b, a = divmod(u, TILES)
             g, t = divmod(a, PACK)
             normed = ring.tile([P, D], BF16)
-            nc.vector.tensor_scalar_mul(out=normed[:], in0=mid_sb[b][:, g, t, :], scalar1=inv_norm[u][:])
+            nc.vector.tensor_scalar_mul(out=normed[:], in0=mid_sb[b][:, g, t, :], scalar1=inv_norm[u])
             mid_n[u] = normed
 
         def tr_mid(u):
-            turned = psum.tile([P, PACK, P], BF16, name="mid_turned", tag="turned")
+            turned = psum.tile([P, PACK, P], BF16, name="mid_turned", tag="pv" if u < TILES and u % PACK >= 2 else "turned")
             for c in range(PACK):
                 nc.tensor.transpose(turned[:, c, :], mid_n[u][:, P * c : P * (c + 1)], ident[:])
             mid_tr[u] = turned
 
-        def copy_mid(u):
+        def copy_mid(u, on_scalar):
             grouped = ring.tile([P, P, PACK], BF16, name="mid_g", align_bytes=64)
-            if u % 2 == 0:
+            if not on_scalar:
                 nc.vector.tensor_copy(out=grouped[:], in_=mid_tr[u][:].rearrange("p c w -> p w c"))
             else:
                 nc.scalar.copy(out=grouped[:], in_=mid_tr[u][:].rearrange("p c w -> p w c"))
@@ -171,7 +191,7 @@ def tile_similarityenhancementmodule_t_kernel(tc, final_features, mid_features, 
                 )
             sim[s] = banks
 
-        def mask_max(s):
+        def mask(s):
             h, j = divmod(s, HALF)
             if j == 0:
                 minus_c = small.tile([P, HALF], F32, name="minus_c")
@@ -179,9 +199,11 @@ def tile_similarityenhancementmodule_t_kernel(tc, final_features, mid_features, 
                 neg_c[h], sums[h] = minus_c, parts
             first = ring.tile([P, P + 2], F32, name="first")
             nc.vector.tensor_tensor(out=first[:, 0:P], in0=sim[s][0][:, 0:P], in1=off_diag[:], op=ALU.mult)
-            nc.vector.tensor_reduce(out=first[:, P : P + 1], in_=sim[s][0][:, P:BANK], axis=AXIS.X, op=ALU.max)
-            nc.vector.tensor_reduce(out=first[:, P + 1 : P + 2], in_=sim[s][1][:], axis=AXIS.X, op=ALU.max)
             head[s] = first
+
+        def max_bank(s, h):
+            columns = sim[s][h][:, P:BANK] if h == 0 else sim[s][h][:]
+            nc.vector.tensor_reduce(out=head[s][:, P + h : P + h + 1], in_=columns, axis=AXIS.X, op=ALU.max)
 
         def row_max(s):
             h, j = divmod(s, HALF)
@@ -248,7 +270,7 @@ def tile_similarityenhancementmodule_t_kernel(tc, final_features, mid_features, 
 
         def pv(s):
             b = s // TILES
-            total = psum.tile([P, D], F32, name="pv_total")
+            total = psum.tile([P, D], F32, name="pv_total", tag="pv")
             for g in range(G):
                 nc.tensor.matmul_mx(
                     out=total[:],
@@ -286,31 +308,76 @@ def tile_similarityenhancementmodule_t_kernel(tc, final_features, mid_features, 
             if s % 2 == 1:
                 nc.sync.dma_start(out=token_view(out[b])[:, g, t - 1 : t + 1, :], in_=blended[s // 2][:])
 
-        def run(stage, index, count):
-            if 0 <= index < count:
-                stage(index)
+        def run(stage, index, first, last, *args):
+            if first <= index < last:
+                stage(index, *args)
 
-        for i in range(-MID_AHEAD, ROWS + PV_BEHIND + 2):
+        for half in range(G):
+            u = PACK * half
+            square(u, True)
+            square(u + 2, False)
+            square(u + 1, True)
+            square(u + 3, False)
+            norm(u)
+        square(TILES, True)
+        for u in range(PACK):
+            scale(u)
+            tr_mid(u)
+        regroup_fin(0)
+        square(TILES + 1, True)
+        for u in range(PACK):
+            copy_mid(u, True)
+        for u in range(PACK, TILES):
+            scale(u)
+            tr_mid(u)
+        quant_mid(0)
+        quant_mid(1)
+        copy_mid(4, True)
+        copy_mid(5, False)
+        quant_mid(2)
+        quant_mid(3)
+        copy_mid(6, True)
+        copy_mid(7, False)
+        quant_mid(4)
+        quant_fin(0)
+        quant_mid(6)
+        quant_mid(5)
+        quant_mid(7)
+
+        for i in range(FIRST, ROWS + PV_BEHIND + 2):
             done_half = i // HALF - 1 if i % HALF == 0 else -1
-            run(tr_e, i - 1, ROWS)
-            run(copy_mid, i + MID_AHEAD - 5, ROWS)
-            run(tr_mid, i + MID_AHEAD - 4, ROWS)
-            run(mask_max, i + 1, ROWS)
-            run(add_sums, done_half, ROWS // HALF)
-            run(exp_rows, i, ROWS)
-            run(sim_rows, i + 2, ROWS)
-            run(copy_e, i - 1, ROWS)
-            run(pv, i - PV_BEHIND, ROWS)
-            run(blend, i - PV_BEHIND - 1, ROWS)
-            run(invert_sums, done_half, ROWS // HALF)
-            run(row_max, i + 1, ROWS)
-            run(gains, done_half, ROWS // HALF)
-            run(square, i + MID_AHEAD, ROWS)
-            run(scale, i + MID_AHEAD - 3, ROWS)
-            run(quant_mid, i + MID_AHEAD - 6, ROWS)
-            run(regroup_fin, i + FIN_AHEAD, ROWS)
-            run(quant_fin, i + FIN_AHEAD - 1, ROWS)
-            run(quant_e, i - 2, ROWS)
-            run(keep_factor, i + 1, ROWS)
-            run(keep_fin, i + 1, ROWS)
-            run(norm, i + MID_AHEAD - 1, ROWS)
+            if i < -2:
+                pieces = []
+            elif i < 0:
+                pieces = [i + 3]
+            elif i < 3:
+                pieces = [2 * i + 3, 2 * i + 4]
+            else:
+                pieces = [i + FIN_AHEAD]
+            run(tr_e, i - 1, 0, ROWS)
+            run(tr_mid, i + MID_AHEAD - 3, TILES, ROWS)
+            run(add_sums, done_half, 0, ROWS // HALF)
+            run(mask, i + 1, 0, ROWS)
+            run(invert_sums, done_half, 0, ROWS // HALF)
+            run(max_bank, i + 1, 0, ROWS, 0)
+            run(gains, done_half, 0, ROWS // HALF)
+            run(max_bank, i + 1, 0, ROWS, 1)
+            run(exp_rows, i, 0, ROWS)
+            run(pv, i - PV_BEHIND, 0, ROWS)
+            run(sim_rows, i + 2, 0, ROWS)
+            run(copy_mid, i + MID_AHEAD - 3, TILES, ROWS, True)
+            run(copy_e, i - 1, 0, ROWS)
+            run(square, i + MID_AHEAD, TILES + 2, ROWS, True)
+            if i % 2 != 0:
+                run(norm, i + MID_AHEAD - 2, TILES, ROWS)
+            run(blend, i - PV_BEHIND - 1, 0, ROWS)
+            run(row_max, i + 1, 0, ROWS)
+            run(scale, i + MID_AHEAD - 2, TILES, ROWS)
+            for u in pieces:
+                run(regroup_fin, u, 0, ROWS)
+            run(quant_e, i - 2, 0, ROWS)
+            run(quant_mid, i + MID_AHEAD - 3, TILES, ROWS)
+            for u in pieces:
+                run(quant_fin, u, 0, ROWS)
+            run(keep_factor, i + 1, 0, ROWS)
+            run(keep_fin, i + 1, 0, ROWS)

@@ -17,6 +17,7 @@ N = 1024
 D = 512
 P = 128
 PACK = 4
+PAIR = 2
 K_PASS = P * PACK
 TILES = N // P
 G = N // K_PASS
@@ -25,7 +26,7 @@ HALF = PACK
 ROWS = B * TILES
 EPS = 1e-12
 
-MID_AHEAD = 13
+MID_AHEAD = 14
 FIN_AHEAD = 6
 PV_BEHIND = 3
 FIRST = -3
@@ -46,32 +47,31 @@ def tile_similarityenhancementmodule_t_kernel(tc, final_features, mid_features, 
         psum = stack.enter_context(tc.psum_pool(name="psum", bufs=2))
 
         def token_view(dram_batch):
-            return dram_batch.rearrange("(g p t) d -> p g t d", g=G, p=P, t=PACK)
+            return dram_batch.rearrange("(a p) d -> p a d", p=P)
 
-        mid_sb = []
-        fin_sb = []
+        mid_sb = [loads.tile([P, TILES, D], BF16, name="mid_t") for b in range(B)]
+        fin_sb = [loads.tile([P, TILES, D], BF16, name="fin_t") for b in range(B)]
+        key_sb = [loads.tile([P, G, PACK, D], BF16, name="key_t") for b in range(B)]
 
-        def load_mid(b):
-            mid_t = loads.tile([P, G, PACK, D], BF16, name="mid_t")
-            for g in range(G):
-                for t in range(0, PACK, 2 if b == 0 and g == 0 else PACK):
-                    last = t + 2 if b == 0 and g == 0 else PACK
-                    nc.sync.dma_start(out=mid_t[:, g, t:last, :], in_=token_view(mid_features[b])[:, g, t:last, :])
-            mid_sb.append(mid_t)
+        def load_tiles(to, dram, b, first, last):
+            nc.sync.dma_start(out=to[b][:, first:last, :], in_=token_view(dram[b])[:, first:last, :])
 
-        def load_fin(b):
-            fin_t = loads.tile([P, G, PACK, D], BF16, name="fin_t")
-            nc.sync.dma_start(out=fin_t[:], in_=token_view(final_features[b]))
-            fin_sb.append(fin_t)
+        def load_keys(b, g):
+            view = final_features[b].rearrange("(g p t) d -> p g t d", g=G, p=P, t=PACK)
+            nc.sync.dma_start(out=key_sb[b][:, g, :, :], in_=view[:, g, :, :])
 
-        load_mid(0)
+        load_tiles(mid_sb, mid_features, 0, 0, 2)
+        load_tiles(mid_sb, mid_features, 0, 2, 4)
+        load_tiles(mid_sb, mid_features, 0, 4, 8)
         for b in range(B):
             if b + 1 < B:
-                load_mid(b + 1)
-            load_fin(b)
+                load_tiles(mid_sb, mid_features, b + 1, 0, 4)
+            load_keys(b, 0)
+            load_keys(b, 1)
+            load_tiles(fin_sb, final_features, b, 0, 8)
+            if b + 1 < B:
+                load_tiles(mid_sb, mid_features, b + 1, 4, 8)
 
-        ident = const.tile([P, P], BF16)
-        make_identity(nc, ident[:])
         ident_f = const.tile([P, P], F32)
         make_identity(nc, ident_f[:])
         off_diag = const.tile([P, P], F32)
@@ -80,6 +80,9 @@ def tile_similarityenhancementmodule_t_kernel(tc, final_features, mid_features, 
         )
         neg_half = const.tile([P, PACK], F32)
         nc.vector.memset(neg_half[:], -0.5)
+        sums_ring = [const.tile([P, HALF, 4], F32, name="sums%d" % k) for k in range(3)]
+        for k in range(3):
+            nc.vector.memset(sums_ring[k][:], 0.0)
 
         sumsq, inv_norm, mid_n, mid_tr, mid_grouped = {}, {}, {}, {}, {}
         mid_codes, mid_scales, fin_codes, fin_scales, fin_grouped = {}, {}, {}, {}, {}
@@ -92,13 +95,12 @@ def tile_similarityenhancementmodule_t_kernel(tc, final_features, mid_features, 
 
         def square(u, on_scalar):
             b, a = divmod(u, TILES)
-            g, t = divmod(a, PACK)
             first, size = group_of(u)
             if first not in sumsq:
                 total = small.tile([P, PACK], F32, name="total")
                 sumsq[first] = total
             squares = ring.tile([P, D], BF16, name="squares")
-            one = mid_sb[b][:, g, t, :]
+            one = mid_sb[b][:, a, :]
             to = sumsq[first][:, u - first : u - first + 1]
             if on_scalar:
                 nc.scalar.activation(out=squares[:], in_=one, func=FUNC.Square, accum_out=to)
@@ -120,23 +122,24 @@ def tile_similarityenhancementmodule_t_kernel(tc, final_features, mid_features, 
 
         def scale(u):
             b, a = divmod(u, TILES)
-            g, t = divmod(a, PACK)
-            normed = ring.tile([P, D], BF16)
-            nc.vector.tensor_scalar_mul(out=normed[:], in0=mid_sb[b][:, g, t, :], scalar1=inv_norm[u])
+            normed = ring.tile([P, D], BF16, name="normed", align_bytes=64)
+            nc.vector.tensor_scalar_mul(out=normed[:], in0=mid_sb[b][:, a, :], scalar1=inv_norm[u])
             mid_n[u] = normed
 
         def tr_mid(u):
-            turned = psum.tile([P, PACK, P], BF16, name="mid_turned", tag="pv" if u < TILES and u % PACK >= 2 else "turned")
-            for c in range(PACK):
-                nc.tensor.transpose(turned[:, c, :], mid_n[u][:, P * c : P * (c + 1)], ident[:])
+            turned = psum.tile([P, PAIR, P], F32, name="mid_turned", tag="pv" if u < TILES and u % PACK >= 2 else "turned")
+            words = mid_n[u][:].bitcast(F32)
+            for w in range(PAIR):
+                nc.tensor.transpose(turned[:, w, :], words[:, w : D // PAIR : PAIR], ident_f[:])
             mid_tr[u] = turned
 
         def copy_mid(u, on_scalar):
             grouped = ring.tile([P, P, PACK], BF16, name="mid_g", align_bytes=64)
-            if not on_scalar:
-                nc.vector.tensor_copy(out=grouped[:], in_=mid_tr[u][:].rearrange("p c w -> p w c"))
+            to = grouped[:].bitcast(F32)
+            if on_scalar:
+                nc.scalar.copy(out=to, in_=mid_tr[u][:].rearrange("p w m -> p m w"))
             else:
-                nc.scalar.copy(out=grouped[:], in_=mid_tr[u][:].rearrange("p c w -> p w c"))
+                nc.vector.tensor_copy(out=to, in_=mid_tr[u][:].rearrange("p w m -> p m w"))
             mid_grouped[u] = grouped
 
         def quant_mid(u):
@@ -148,7 +151,7 @@ def tile_similarityenhancementmodule_t_kernel(tc, final_features, mid_features, 
             nc.vector.quantize_mx(
                 out=mid_codes[b][:, P * a : P * (a + 1)].bitcast(FP8X4),
                 scales=mid_scales[b][:, P * a : P * (a + 1)],
-                in_=mid_grouped[u][:].rearrange("p w c -> p (w c)"),
+                in_=mid_grouped[u][:].rearrange("p m c -> p (m c)"),
             )
 
         def regroup_fin(u):
@@ -157,7 +160,7 @@ def tile_similarityenhancementmodule_t_kernel(tc, final_features, mid_features, 
             grouped = ring.tile([P, P, PACK], BF16, name="fin_g", align_bytes=64)
             nc.vector.tensor_copy(
                 out=grouped[:].rearrange("p (c i) t -> p c t i", i=4),
-                in_=fin_sb[b][:, g, :, P * q : P * (q + 1)].rearrange("p t (c i) -> p c t i", i=4),
+                in_=key_sb[b][:, g, :, P * q : P * (q + 1)].rearrange("p t (c i) -> p c t i", i=4),
             )
             fin_grouped[u] = grouped
 
@@ -176,27 +179,32 @@ def tile_similarityenhancementmodule_t_kernel(tc, final_features, mid_features, 
 
         def sim_rows(s):
             b, a = divmod(s, TILES)
+            own = a // PACK
             banks = [psum.tile([P, BANK], F32, name="sim%d" % h) for h in range(2)]
-            for nb in range(TILES):
-                kb = (a + nb) % TILES
-                h, q = divmod(nb, PACK)
+
+            def product(to, first, last):
                 nc.tensor.matmul_mx(
-                    out=banks[h][:, P * q : P * (q + 1)],
+                    out=to,
                     lhsT=mid_codes[b][:, P * a : P * (a + 1)].bitcast(FP8X4),
                     lhsT_scale=mid_scales[b][:, P * a : P * (a + 1)],
-                    rhs=mid_codes[b][:, P * kb : P * (kb + 1)].bitcast(FP8X4),
-                    rhs_scale=mid_scales[b][:, P * kb : P * (kb + 1)],
+                    rhs=mid_codes[b][:, P * first : P * last].bitcast(FP8X4),
+                    rhs_scale=mid_scales[b][:, P * first : P * last],
                     start=True,
                     stop=True,
                 )
+
+            order = [a] + [k for k in range(PACK * own, PACK * (own + 1)) if k != a]
+            for q, k in enumerate(order):
+                product(banks[0][:, P * q : P * (q + 1)], k, k + 1)
+            other = 1 - own
+            product(banks[1][:], PACK * other, PACK * (other + 1))
             sim[s] = banks
 
         def mask(s):
             h, j = divmod(s, HALF)
             if j == 0:
                 minus_c = small.tile([P, HALF], F32, name="minus_c")
-                parts = small.tile([P, HALF, 3], F32, name="parts")
-                neg_c[h], sums[h] = minus_c, parts
+                neg_c[h], sums[h] = minus_c, sums_ring[h % 3]
             first = ring.tile([P, P + 2], F32, name="first")
             nc.vector.tensor_tensor(out=first[:, 0:P], in0=sim[s][0][:, 0:P], in1=off_diag[:], op=ALU.mult)
             head[s] = first
@@ -210,31 +218,36 @@ def tile_similarityenhancementmodule_t_kernel(tc, final_features, mid_features, 
             nc.vector.tensor_reduce(out=neg_c[h][:, j : j + 1], in_=head[s][:], axis=AXIS.X, op=ALU.max, negate=True)
 
         def exp_rows(s):
+            a = s % TILES
+            own, mine = divmod(a, PACK)
             h, j = divmod(s, HALF)
-            e = ring.tile([P, N], BF16, name="e")
-            bias = neg_c[h][:, j : j + 1]
-            nc.scalar.activation(
-                out=e[:, 0:P], in_=head[s][:, 0:P], func=FUNC.Exp, bias=bias, accum_out=sums[h][:, j, 0:1]
-            )
-            nc.scalar.activation(
-                out=e[:, P:BANK], in_=sim[s][0][:, P:BANK], func=FUNC.Exp, bias=bias, accum_out=sums[h][:, j, 1:2]
-            )
-            nc.scalar.activation(
-                out=e[:, BANK:N], in_=sim[s][1][:], func=FUNC.Exp, bias=bias, accum_out=sums[h][:, j, 2:3]
-            )
+            e = ring.tile([P, G, PAIR, P, PAIR], BF16, name="e", align_bytes=64)
+            parts = [(head[s][:, 0:P], own, mine, mine + 1)]
+            if mine > 0:
+                parts.append((sim[s][0][:, P : P * (mine + 1)], own, 0, mine))
+            if mine < PACK - 1:
+                parts.append((sim[s][0][:, P * (mine + 1) : BANK], own, mine + 1, PACK))
+            parts.append((sim[s][1][:], 1 - own, 0, PACK))
+            share = P // PACK
+            for n, (columns, g, first, last) in enumerate(parts):
+                nc.scalar.activation(
+                    out=e[:, g, :, share * first : share * last, :],
+                    in_=columns.rearrange("q (p w i) -> q w p i", w=PAIR, i=PAIR),
+                    func=FUNC.Exp, bias=neg_c[h][:, j : j + 1], accum_out=sums[h][:, j, n : n + 1],
+                )
             e_row[s] = e
 
         def tr_e(s):
-            a = s % TILES
-            turned = psum.tile([P, TILES, P], BF16, name="e_turned", tag="turned")
-            for nb in range(TILES):
-                kb = (a + nb) % TILES
-                nc.tensor.transpose(turned[:, kb, :], e_row[s][:, P * nb : P * (nb + 1)], ident[:])
+            turned = psum.tile([P, G, PAIR, P], F32, name="e_turned", tag="turned")
+            for g in range(G):
+                for w in range(PAIR):
+                    words = e_row[s][:, g, w, :, :].rearrange("q p i -> q (p i)").bitcast(F32)
+                    nc.tensor.transpose(turned[:, g, w, :], words, ident_f[:])
             e_tr[s] = turned
 
         def copy_e(s):
             grouped = ring.tile([P, G, P, PACK], BF16, name="e_g", align_bytes=64)
-            nc.scalar.copy(out=grouped[:], in_=e_tr[s][:].rearrange("p (g t) w -> p g w t", g=G))
+            nc.scalar.copy(out=grouped[:].bitcast(F32), in_=e_tr[s][:].rearrange("p g w m -> p g m w"))
             e_grouped[s] = grouped
 
         def quant_e(s):
@@ -285,18 +298,15 @@ def tile_similarityenhancementmodule_t_kernel(tc, final_features, mid_features, 
 
         def keep_fin(s):
             b, a = divmod(s, TILES)
-            g, t = divmod(a, PACK)
-            h, j = divmod(s, HALF)
             part = late.tile([P, D], F32, name="part")
             nc.gpsimd.tensor_scalar(
-                out=part[:], in0=fin_sb[b][:, g, t, :], scalar1=keep[s][:], scalar2=0.0,
+                out=part[:], in0=fin_sb[b][:, a, :], scalar1=keep[s][:], scalar2=0.0,
                 op0=ALU.mult, op1=ALU.add,
             )
             kept[s] = part
 
         def blend(s):
             b, a = divmod(s, TILES)
-            g, t = divmod(a, PACK)
             h, j = divmod(s, HALF)
             if s % 2 == 0:
                 pair = ring.tile([P, 2, D], F32, name="pair")
@@ -306,7 +316,7 @@ def tile_similarityenhancementmodule_t_kernel(tc, final_features, mid_features, 
                 op0=ALU.mult, op1=ALU.add,
             )
             if s % 2 == 1:
-                nc.sync.dma_start(out=token_view(out[b])[:, g, t - 1 : t + 1, :], in_=blended[s // 2][:])
+                nc.sync.dma_start(out=token_view(out[b])[:, a - 1 : a + 1, :], in_=blended[s // 2][:])
 
         def run(stage, index, first, last, *args):
             if first <= index < last:
@@ -320,11 +330,11 @@ def tile_similarityenhancementmodule_t_kernel(tc, final_features, mid_features, 
             square(u + 3, False)
             norm(u)
         square(TILES, True)
+        square(TILES + 1, True)
+        norm(TILES)
         for u in range(PACK):
             scale(u)
             tr_mid(u)
-        regroup_fin(0)
-        square(TILES + 1, True)
         for u in range(PACK):
             copy_mid(u, True)
         for u in range(PACK, TILES):
@@ -339,10 +349,12 @@ def tile_similarityenhancementmodule_t_kernel(tc, final_features, mid_features, 
         copy_mid(6, True)
         copy_mid(7, False)
         quant_mid(4)
-        quant_fin(0)
         quant_mid(6)
         quant_mid(5)
+        regroup_fin(0)
         quant_mid(7)
+        quant_fin(0)
+        square(TILES + 2, True)
 
         for i in range(FIRST, ROWS + PV_BEHIND + 2):
             done_half = i // HALF - 1 if i % HALF == 0 else -1
@@ -355,7 +367,7 @@ def tile_similarityenhancementmodule_t_kernel(tc, final_features, mid_features, 
             else:
                 pieces = [i + FIN_AHEAD]
             run(tr_e, i - 1, 0, ROWS)
-            run(tr_mid, i + MID_AHEAD - 3, TILES, ROWS)
+            run(tr_mid, i + MID_AHEAD - 4, TILES, ROWS)
             run(add_sums, done_half, 0, ROWS // HALF)
             run(mask, i + 1, 0, ROWS)
             run(invert_sums, done_half, 0, ROWS // HALF)
@@ -365,18 +377,18 @@ def tile_similarityenhancementmodule_t_kernel(tc, final_features, mid_features, 
             run(exp_rows, i, 0, ROWS)
             run(pv, i - PV_BEHIND, 0, ROWS)
             run(sim_rows, i + 2, 0, ROWS)
-            run(copy_mid, i + MID_AHEAD - 3, TILES, ROWS, True)
+            run(copy_mid, i + MID_AHEAD - 4, TILES, ROWS, True)
             run(copy_e, i - 1, 0, ROWS)
-            run(square, i + MID_AHEAD, TILES + 2, ROWS, True)
-            if i % 2 != 0:
-                run(norm, i + MID_AHEAD - 2, TILES, ROWS)
+            run(square, i + MID_AHEAD, TILES + 3, ROWS, True)
+            if i % 2 == 0:
+                run(norm, i + MID_AHEAD - 2, TILES + 2, ROWS)
             run(blend, i - PV_BEHIND - 1, 0, ROWS)
             run(row_max, i + 1, 0, ROWS)
-            run(scale, i + MID_AHEAD - 2, TILES, ROWS)
+            run(scale, i + MID_AHEAD - 3, TILES, ROWS)
             for u in pieces:
                 run(regroup_fin, u, 0, ROWS)
             run(quant_e, i - 2, 0, ROWS)
-            run(quant_mid, i + MID_AHEAD - 3, TILES, ROWS)
+            run(quant_mid, i + MID_AHEAD - 4, TILES, ROWS)
             for u in pieces:
                 run(quant_fin, u, 0, ROWS)
             run(keep_factor, i + 1, 0, ROWS)

@@ -26,7 +26,7 @@ HALF = PACK
 ROWS = B * TILES
 EPS = 1e-12
 
-MID_AHEAD = 14
+MID_AHEAD = 16
 FIN_AHEAD = 6
 PV_BEHIND = 3
 FIRST = -3
@@ -64,9 +64,9 @@ def tile_similarityenhancementmodule_t_kernel(tc, final_features, mid_features, 
         load_tiles(mid_sb, mid_features, 0, 2, 4)
         load_tiles(mid_sb, mid_features, 0, 4, 8)
         for b in range(B):
+            load_keys(b, 0)
             if b + 1 < B:
                 load_tiles(mid_sb, mid_features, b + 1, 0, 4)
-            load_keys(b, 0)
             load_keys(b, 1)
             load_tiles(fin_sb, final_features, b, 0, 8)
             if b + 1 < B:
@@ -80,6 +80,8 @@ def tile_similarityenhancementmodule_t_kernel(tc, final_features, mid_features, 
         )
         neg_half = const.tile([P, PACK], F32)
         nc.vector.memset(neg_half[:], -0.5)
+        one = const.tile([P, 1], F32)
+        nc.vector.memset(one[:], 1.0)
         sums_ring = [const.tile([P, HALF, 4], F32, name="sums%d" % k) for k in range(3)]
         for k in range(3):
             nc.vector.memset(sums_ring[k][:], 0.0)
@@ -90,7 +92,7 @@ def tile_similarityenhancementmodule_t_kernel(tc, final_features, mid_features, 
         row_sum, inv_sum, gain, keep, acc, kept, blended = {}, {}, {}, {}, {}, {}, {}
 
         def group_of(u):
-            size = PACK if u < TILES else 2
+            size = PACK
             return u - u % size, size
 
         def square(u, on_scalar):
@@ -100,13 +102,13 @@ def tile_similarityenhancementmodule_t_kernel(tc, final_features, mid_features, 
                 total = small.tile([P, PACK], F32, name="total")
                 sumsq[first] = total
             squares = ring.tile([P, D], BF16, name="squares")
-            one = mid_sb[b][:, a, :]
+            tile_u = mid_sb[b][:, a, :]
             to = sumsq[first][:, u - first : u - first + 1]
             if on_scalar:
-                nc.scalar.activation(out=squares[:], in_=one, func=FUNC.Square, accum_out=to)
+                nc.scalar.activation(out=squares[:], in_=tile_u, func=FUNC.Square, accum_out=to)
             else:
                 nc.vector.scalar_tensor_tensor(
-                    out=squares[:], in0=one, scalar=1.0, in1=one, op0=ALU.mult, op1=ALU.mult, accum_out=to
+                    out=squares[:], in0=tile_u, scalar=1.0, in1=tile_u, op0=ALU.mult, op1=ALU.mult, accum_out=to
                 )
 
         def norm(u):
@@ -158,10 +160,12 @@ def tile_similarityenhancementmodule_t_kernel(tc, final_features, mid_features, 
             b, r = divmod(u, TILES)
             g, q = divmod(r, PACK)
             grouped = ring.tile([P, P, PACK], BF16, name="fin_g", align_bytes=64)
-            nc.vector.tensor_copy(
-                out=grouped[:].rearrange("p (c i) t -> p c t i", i=4),
-                in_=key_sb[b][:, g, :, P * q : P * (q + 1)].rearrange("p t (c i) -> p c t i", i=4),
-            )
+            to = grouped[:].rearrange("p (c i) t -> p c t i", i=4)
+            rows = key_sb[b][:, g, :, P * q : P * (q + 1)].rearrange("p t (c i) -> p c t i", i=4)
+            if u >= TILES and u % 3 == 2:
+                nc.scalar.copy(out=to, in_=rows)
+            else:
+                nc.vector.tensor_copy(out=to, in_=rows)
             fin_grouped[u] = grouped
 
         def quant_fin(u):
@@ -278,7 +282,7 @@ def tile_similarityenhancementmodule_t_kernel(tc, final_features, mid_features, 
         def keep_factor(s):
             h, j = divmod(s, HALF)
             one_minus_c = small.tile([P, 1], F32)
-            nc.vector.tensor_scalar_add(out=one_minus_c[:], in0=neg_c[h][:, j : j + 1], scalar1=1.0)
+            nc.scalar.activation(out=one_minus_c[:], in_=neg_c[h][:, j : j + 1], func=FUNC.Identity, bias=one[:])
             keep[s] = one_minus_c
 
         def pv(s):
@@ -331,12 +335,15 @@ def tile_similarityenhancementmodule_t_kernel(tc, final_features, mid_features, 
             norm(u)
         square(TILES, True)
         square(TILES + 1, True)
-        norm(TILES)
+        square(TILES + 2, True)
+        regroup_fin(0)
         for u in range(PACK):
             scale(u)
             tr_mid(u)
         for u in range(PACK):
             copy_mid(u, True)
+        square(TILES + 3, True)
+        norm(TILES)
         for u in range(PACK, TILES):
             scale(u)
             tr_mid(u)
@@ -351,45 +358,46 @@ def tile_similarityenhancementmodule_t_kernel(tc, final_features, mid_features, 
         quant_mid(4)
         quant_mid(6)
         quant_mid(5)
-        regroup_fin(0)
-        quant_mid(7)
         quant_fin(0)
-        square(TILES + 2, True)
+        quant_mid(7)
+        square(TILES + 4, True)
 
+        late_pieces = []
         for i in range(FIRST, ROWS + PV_BEHIND + 2):
-            done_half = i // HALF - 1 if i % HALF == 0 else -1
+            done_half = i // HALF if i % HALF == HALF - 1 else -1
             if i < -2:
                 pieces = []
-            elif i < 0:
-                pieces = [i + 3]
-            elif i < 3:
-                pieces = [2 * i + 3, 2 * i + 4]
+            elif i < -1:
+                pieces = [1]
+            elif i < 2:
+                pieces = [2 * i + 4, 2 * i + 5]
             else:
                 pieces = [i + FIN_AHEAD]
             run(tr_e, i - 1, 0, ROWS)
-            run(tr_mid, i + MID_AHEAD - 4, TILES, ROWS)
-            run(add_sums, done_half, 0, ROWS // HALF)
+            run(tr_mid, i + MID_AHEAD - 6, TILES, ROWS)
             run(mask, i + 1, 0, ROWS)
-            run(invert_sums, done_half, 0, ROWS // HALF)
             run(max_bank, i + 1, 0, ROWS, 0)
-            run(gains, done_half, 0, ROWS // HALF)
             run(max_bank, i + 1, 0, ROWS, 1)
             run(exp_rows, i, 0, ROWS)
             run(pv, i - PV_BEHIND, 0, ROWS)
             run(sim_rows, i + 2, 0, ROWS)
-            run(copy_mid, i + MID_AHEAD - 4, TILES, ROWS, True)
+            run(copy_mid, i + MID_AHEAD - 6, TILES, ROWS, True)
+            run(square, i + MID_AHEAD, TILES + 5, ROWS, True)
             run(copy_e, i - 1, 0, ROWS)
-            run(square, i + MID_AHEAD, TILES + 3, ROWS, True)
-            if i % 2 == 0:
-                run(norm, i + MID_AHEAD - 2, TILES + 2, ROWS)
+            if i % PACK == 0:
+                run(norm, i + MID_AHEAD - 4, TILES + 4, ROWS)
             run(blend, i - PV_BEHIND - 1, 0, ROWS)
-            run(row_max, i + 1, 0, ROWS)
-            run(scale, i + MID_AHEAD - 3, TILES, ROWS)
+            run(scale, i + MID_AHEAD - 5, TILES, ROWS)
+            run(add_sums, done_half, 0, ROWS // HALF)
             for u in pieces:
                 run(regroup_fin, u, 0, ROWS)
             run(quant_e, i - 2, 0, ROWS)
-            run(quant_mid, i + MID_AHEAD - 4, TILES, ROWS)
-            for u in pieces:
+            run(invert_sums, done_half, 0, ROWS // HALF)
+            run(quant_mid, i + MID_AHEAD - 6, TILES, ROWS)
+            for u in late_pieces:
                 run(quant_fin, u, 0, ROWS)
+            late_pieces = pieces
+            run(row_max, i + 1, 0, ROWS)
+            run(gains, done_half, 0, ROWS // HALF)
             run(keep_factor, i + 1, 0, ROWS)
             run(keep_fin, i + 1, 0, ROWS)

@@ -26,8 +26,8 @@ HALF = PACK
 ROWS = B * TILES
 EPS = 1e-12
 
-MID_AHEAD = 16
-FIN_AHEAD = 6
+MID_AHEAD = 17
+FIN_AHEAD = 5
 PV_BEHIND = 3
 FIRST = -3
 
@@ -62,11 +62,13 @@ def tile_similarityenhancementmodule_t_kernel(tc, final_features, mid_features, 
 
         load_tiles(mid_sb, mid_features, 0, 0, 2)
         load_tiles(mid_sb, mid_features, 0, 2, 4)
+        load_keys(0, 0)
         load_tiles(mid_sb, mid_features, 0, 4, 8)
         for b in range(B):
-            load_keys(b, 0)
             if b + 1 < B:
                 load_tiles(mid_sb, mid_features, b + 1, 0, 4)
+            if b > 0:
+                load_keys(b, 0)
             load_keys(b, 1)
             load_tiles(fin_sb, final_features, b, 0, 8)
             if b + 1 < B:
@@ -80,8 +82,6 @@ def tile_similarityenhancementmodule_t_kernel(tc, final_features, mid_features, 
         )
         neg_half = const.tile([P, PACK], F32)
         nc.vector.memset(neg_half[:], -0.5)
-        one = const.tile([P, 1], F32)
-        nc.vector.memset(one[:], 1.0)
         sums_ring = [const.tile([P, HALF, 4], F32, name="sums%d" % k) for k in range(3)]
         for k in range(3):
             nc.vector.memset(sums_ring[k][:], 0.0)
@@ -156,16 +156,21 @@ def tile_similarityenhancementmodule_t_kernel(tc, final_features, mid_features, 
                 in_=mid_grouped[u][:].rearrange("p m c -> p (m c)"),
             )
 
-        def regroup_fin(u):
+        def regroup_fin(u, on_gpsimd):
             b, r = divmod(u, TILES)
             g, q = divmod(r, PACK)
             grouped = ring.tile([P, P, PACK], BF16, name="fin_g", align_bytes=64)
-            to = grouped[:].rearrange("p (c i) t -> p c t i", i=4)
-            rows = key_sb[b][:, g, :, P * q : P * (q + 1)].rearrange("p t (c i) -> p c t i", i=4)
-            if u >= TILES and u % 3 == 2:
-                nc.scalar.copy(out=to, in_=rows)
+            rows = key_sb[b][:, g, :, P * q : P * (q + 1)]
+            if on_gpsimd:
+                nc.gpsimd.tensor_scalar(
+                    out=grouped[:], in0=rows.rearrange("p t d -> p d t"), scalar1=1.0, scalar2=0.0,
+                    op0=ALU.mult, op1=ALU.add,
+                )
             else:
-                nc.vector.tensor_copy(out=to, in_=rows)
+                nc.vector.tensor_copy(
+                    out=grouped[:].rearrange("p (c i) t -> p c t i", i=4),
+                    in_=rows.rearrange("p t (c i) -> p c t i", i=4),
+                )
             fin_grouped[u] = grouped
 
         def quant_fin(u):
@@ -282,7 +287,7 @@ def tile_similarityenhancementmodule_t_kernel(tc, final_features, mid_features, 
         def keep_factor(s):
             h, j = divmod(s, HALF)
             one_minus_c = small.tile([P, 1], F32)
-            nc.scalar.activation(out=one_minus_c[:], in_=neg_c[h][:, j : j + 1], func=FUNC.Identity, bias=one[:])
+            nc.vector.tensor_scalar_add(out=one_minus_c[:], in0=neg_c[h][:, j : j + 1], scalar1=1.0)
             keep[s] = one_minus_c
 
         def pv(s):
@@ -322,82 +327,82 @@ def tile_similarityenhancementmodule_t_kernel(tc, final_features, mid_features, 
             if s % 2 == 1:
                 nc.sync.dma_start(out=token_view(out[b])[:, a - 1 : a + 1, :], in_=blended[s // 2][:])
 
+        def blends(i):
+            return [i - PV_BEHIND - 1] if i > PV_BEHIND else []
+
         def run(stage, index, first, last, *args):
             if first <= index < last:
                 stage(index, *args)
 
         for half in range(G):
             u = PACK * half
-            square(u, True)
-            square(u + 2, False)
-            square(u + 1, True)
             square(u + 3, False)
+            for k in range(3):
+                square(u + k, True)
             norm(u)
+            regroup_fin(2 * half, False)
+            regroup_fin(2 * half + 1, False)
         square(TILES, True)
-        square(TILES + 1, True)
-        square(TILES + 2, True)
-        regroup_fin(0)
         for u in range(PACK):
             scale(u)
             tr_mid(u)
+        quant_fin(0)
+        quant_fin(1)
         for u in range(PACK):
             copy_mid(u, True)
-        square(TILES + 3, True)
-        norm(TILES)
+        square(TILES + 1, True)
         for u in range(PACK, TILES):
             scale(u)
             tr_mid(u)
         quant_mid(0)
         quant_mid(1)
-        copy_mid(4, True)
-        copy_mid(5, False)
+        quant_fin(2)
         quant_mid(2)
+        quant_fin(3)
         quant_mid(3)
-        copy_mid(6, True)
-        copy_mid(7, False)
-        quant_mid(4)
-        quant_mid(6)
-        quant_mid(5)
-        quant_fin(0)
-        quant_mid(7)
+        for u in range(PACK, TILES):
+            copy_mid(u, True)
+        for u in range(PACK, TILES):
+            regroup_fin(u, False)
+            quant_mid(u)
+        square(TILES + 2, True)
+        square(TILES + 3, True)
+        norm(TILES)
         square(TILES + 4, True)
+        square(TILES + 5, True)
+        for u in range(PACK, TILES):
+            quant_fin(u)
+        scale(TILES)
+        tr_mid(TILES)
+        copy_mid(TILES, True)
 
-        late_pieces = []
-        for i in range(FIRST, ROWS + PV_BEHIND + 2):
+        for i in range(FIRST, ROWS + PV_BEHIND):
             done_half = i // HALF if i % HALF == HALF - 1 else -1
-            if i < -2:
-                pieces = []
-            elif i < -1:
-                pieces = [1]
-            elif i < 2:
-                pieces = [2 * i + 4, 2 * i + 5]
-            else:
-                pieces = [i + FIN_AHEAD]
+            fin_here = i + FIN_AHEAD
             run(tr_e, i - 1, 0, ROWS)
-            run(tr_mid, i + MID_AHEAD - 6, TILES, ROWS)
+            run(tr_mid, i + MID_AHEAD - 6, TILES + 1, ROWS)
             run(mask, i + 1, 0, ROWS)
             run(max_bank, i + 1, 0, ROWS, 0)
             run(max_bank, i + 1, 0, ROWS, 1)
             run(exp_rows, i, 0, ROWS)
             run(pv, i - PV_BEHIND, 0, ROWS)
             run(sim_rows, i + 2, 0, ROWS)
-            run(copy_mid, i + MID_AHEAD - 6, TILES, ROWS, True)
-            run(square, i + MID_AHEAD, TILES + 5, ROWS, True)
+            run(copy_mid, i + MID_AHEAD - 6, TILES + 1, ROWS, True)
+            run(square, i + MID_AHEAD, TILES + 6, ROWS, True)
             run(copy_e, i - 1, 0, ROWS)
-            if i % PACK == 0:
+            if (i + 1) % PACK == 0:
                 run(norm, i + MID_AHEAD - 4, TILES + 4, ROWS)
-            run(blend, i - PV_BEHIND - 1, 0, ROWS)
-            run(scale, i + MID_AHEAD - 5, TILES, ROWS)
+            for s in blends(i):
+                blend(s)
+            run(row_max, i + 1, 0, ROWS)
+            run(scale, i + MID_AHEAD - 5, TILES + 1, ROWS)
             run(add_sums, done_half, 0, ROWS // HALF)
-            for u in pieces:
-                run(regroup_fin, u, 0, ROWS)
             run(quant_e, i - 2, 0, ROWS)
             run(invert_sums, done_half, 0, ROWS // HALF)
-            run(quant_mid, i + MID_AHEAD - 6, TILES, ROWS)
-            for u in late_pieces:
-                run(quant_fin, u, 0, ROWS)
-            late_pieces = pieces
-            run(row_max, i + 1, 0, ROWS)
+            run(quant_mid, i + MID_AHEAD - 7, TILES, ROWS)
+            run(quant_fin, fin_here, TILES, ROWS)
             run(gains, done_half, 0, ROWS // HALF)
             run(keep_factor, i + 1, 0, ROWS)
             run(keep_fin, i + 1, 0, ROWS)
+            run(regroup_fin, fin_here + 2, TILES, ROWS, True)
+        blend(ROWS - 1)

@@ -22,11 +22,12 @@ K_PASS = P * PACK
 TILES = N // P
 G = N // K_PASS
 BANK = 512
+LAST = 3
 HALF = PACK
 ROWS = B * TILES
 EPS = 1e-12
 
-MID_AHEAD = 17
+MID_AHEAD = 10
 FIN_AHEAD = 5
 PV_BEHIND = 3
 FIRST = -3
@@ -62,13 +63,11 @@ def tile_similarityenhancementmodule_t_kernel(tc, final_features, mid_features, 
 
         load_tiles(mid_sb, mid_features, 0, 0, 2)
         load_tiles(mid_sb, mid_features, 0, 2, 4)
-        load_keys(0, 0)
         load_tiles(mid_sb, mid_features, 0, 4, 8)
         for b in range(B):
+            load_keys(b, 0)
             if b + 1 < B:
                 load_tiles(mid_sb, mid_features, b + 1, 0, 4)
-            if b > 0:
-                load_keys(b, 0)
             load_keys(b, 1)
             load_tiles(fin_sb, final_features, b, 0, 8)
             if b + 1 < B:
@@ -85,51 +84,67 @@ def tile_similarityenhancementmodule_t_kernel(tc, final_features, mid_features, 
         sums_ring = [const.tile([P, HALF, 4], F32, name="sums%d" % k) for k in range(3)]
         for k in range(3):
             nc.vector.memset(sums_ring[k][:], 0.0)
+        warm = const.tile([P, 1], F32)
+        nc.vector.memset(warm[:], 1.0)
+        nc.scalar.activation(out=warm[:], in_=warm[:], func=FUNC.Sqrt)
 
-        sumsq, inv_norm, mid_n, mid_tr, mid_grouped = {}, {}, {}, {}, {}
+        sumsq, roots, clamped, inv_norm, mid_n, mid_tr, mid_grouped = {}, {}, {}, {}, {}, {}, {}
         mid_codes, mid_scales, fin_codes, fin_scales, fin_grouped = {}, {}, {}, {}, {}
-        sim, head, neg_c, sums, e_row, e_tr, e_grouped, e_codes, e_scales = {}, {}, {}, {}, {}, {}, {}, {}, {}
+        sim, head, neg_c, sums = {}, {}, {}, {}
+        e_row, e_tr, e_grouped, e_codes, e_scales = {}, {}, {}, {}, {}
         row_sum, inv_sum, gain, keep, acc, kept, blended = {}, {}, {}, {}, {}, {}, {}
-
-        def group_of(u):
-            size = PACK
-            return u - u % size, size
 
         def square(u, on_scalar):
             b, a = divmod(u, TILES)
-            first, size = group_of(u)
+            first = u - u % PACK
             if first not in sumsq:
                 total = small.tile([P, PACK], F32, name="total")
                 sumsq[first] = total
             squares = ring.tile([P, D], BF16, name="squares")
-            tile_u = mid_sb[b][:, a, :]
+            tokens = mid_sb[b][:, a, :]
             to = sumsq[first][:, u - first : u - first + 1]
             if on_scalar:
-                nc.scalar.activation(out=squares[:], in_=tile_u, func=FUNC.Square, accum_out=to)
+                nc.scalar.activation(out=squares[:], in_=tokens, func=FUNC.Square, accum_out=to)
             else:
                 nc.vector.scalar_tensor_tensor(
-                    out=squares[:], in0=tile_u, scalar=1.0, in1=tile_u, op0=ALU.mult, op1=ALU.mult, accum_out=to
+                    out=squares[:], in0=tokens, scalar=1.0, in1=tokens, op0=ALU.mult, op1=ALU.mult, accum_out=to
                 )
 
-        def norm(u):
-            first, size = group_of(u)
-            clamped = small.tile([P, PACK], F32, name="clamped")
-            nc.gpsimd.tensor_scalar_max(out=clamped[:, 0:size], in0=sumsq[first][:, 0:size], scalar1=EPS * EPS)
+        def first_roots(u):
+            root = small.tile([P, PACK], F32, name="root")
+            nc.scalar.activation(out=root[:], in_=sumsq[u][:], func=FUNC.Sqrt)
+            roots[u] = root
+
+        def first_norms(u):
+            bounded = small.tile([P, PACK], F32, name="bounded")
+            nc.vector.tensor_scalar_max(out=bounded[:], in0=roots[u][:], scalar1=EPS)
             inverse = small.tile([P, PACK], F32, name="inverse")
-            nc.gpsimd.tensor_tensor(
-                out=inverse[:, 0:size], in0=clamped[:, 0:size], in1=neg_half[:, 0:size], op=ALU.pow
-            )
-            for j in range(size):
-                inv_norm[first + j] = inverse[:, j : j + 1]
+            nc.vector.reciprocal(out=inverse[:], in_=bounded[:])
+            inv_norm[u] = inverse
+
+        def clamp(u):
+            bounded = small.tile([P, PACK], F32, name="bounded")
+            nc.vector.tensor_scalar_max(out=bounded[:], in0=sumsq[u][:], scalar1=EPS * EPS)
+            clamped[u] = bounded
+
+        def norm(u):
+            if u not in clamped:
+                bounded = small.tile([P, PACK], F32, name="bounded")
+                nc.gpsimd.tensor_scalar_max(out=bounded[:], in0=sumsq[u][:], scalar1=EPS * EPS)
+                clamped[u] = bounded
+            inverse = small.tile([P, PACK], F32, name="inverse")
+            nc.gpsimd.tensor_tensor(out=inverse[:], in0=clamped[u][:], in1=neg_half[:], op=ALU.pow)
+            inv_norm[u] = inverse
 
         def scale(u):
             b, a = divmod(u, TILES)
             normed = ring.tile([P, D], BF16, name="normed", align_bytes=64)
-            nc.vector.tensor_scalar_mul(out=normed[:], in0=mid_sb[b][:, a, :], scalar1=inv_norm[u])
+            nc.vector.tensor_scalar_mul(out=normed[:], in0=mid_sb[b][:, a, :], scalar1=inv_norm[u - u % PACK][:, u % PACK : u % PACK + 1])
             mid_n[u] = normed
 
         def tr_mid(u):
-            turned = psum.tile([P, PAIR, P], F32, name="mid_turned", tag="pv" if u < TILES and u % PACK >= 2 else "turned")
+            early = u < TILES and u % PACK >= PAIR or TILES <= u < 2 * TILES and u % 2 == 1
+            turned = psum.tile([P, PAIR, P], F32, name="mid_turned", tag="pv" if early else "turned")
             words = mid_n[u][:].bitcast(F32)
             for w in range(PAIR):
                 nc.tensor.transpose(turned[:, w, :], words[:, w : D // PAIR : PAIR], ident_f[:])
@@ -156,12 +171,14 @@ def tile_similarityenhancementmodule_t_kernel(tc, final_features, mid_features, 
                 in_=mid_grouped[u][:].rearrange("p m c -> p (m c)"),
             )
 
-        def regroup_fin(u, on_gpsimd):
+        def regroup_fin(u, engine):
             b, r = divmod(u, TILES)
             g, q = divmod(r, PACK)
-            grouped = ring.tile([P, P, PACK], BF16, name="fin_g", align_bytes=64)
+            grouped = ring.tile([P, P, PACK], BF16, name="fin_g", tag="fin_" + engine, align_bytes=64, bufs=2)
             rows = key_sb[b][:, g, :, P * q : P * (q + 1)]
-            if on_gpsimd:
+            if engine == "S":
+                nc.scalar.copy(out=grouped[:], in_=rows.rearrange("p t d -> p d t"))
+            elif engine == "G":
                 nc.gpsimd.tensor_scalar(
                     out=grouped[:], in0=rows.rearrange("p t d -> p d t"), scalar1=1.0, scalar2=0.0,
                     op0=ALU.mult, op1=ALU.add,
@@ -263,7 +280,7 @@ def tile_similarityenhancementmodule_t_kernel(tc, final_features, mid_features, 
             words = late.tile([P, G * P], U32, name="e_words", align_bytes=64)
             plane = late.tile([P, G * P], U8, name="e_plane", align_bytes=64)
             nc.vector.quantize_mx(
-                out=words[:].bitcast(FP8X4), scales=plane[:], in_=e_grouped[s][:].rearrange("p g w t -> p (g w t)")
+                out=words[:].bitcast(FP8X4), scales=plane[:], in_=e_grouped[s][:].rearrange("p g m t -> p (g m t)")
             )
             e_codes[s], e_scales[s] = words, plane
 
@@ -284,11 +301,10 @@ def tile_similarityenhancementmodule_t_kernel(tc, final_features, mid_features, 
             )
             gain[h] = c_over_sum
 
-        def keep_factor(s):
-            h, j = divmod(s, HALF)
-            one_minus_c = small.tile([P, 1], F32)
-            nc.vector.tensor_scalar_add(out=one_minus_c[:], in0=neg_c[h][:, j : j + 1], scalar1=1.0)
-            keep[s] = one_minus_c
+        def keep_factors(h):
+            one_minus_c = small.tile([P, HALF], F32)
+            nc.vector.tensor_scalar_add(out=one_minus_c[:], in0=neg_c[h][:], scalar1=1.0)
+            keep[h] = one_minus_c
 
         def pv(s):
             b = s // TILES
@@ -307,11 +323,18 @@ def tile_similarityenhancementmodule_t_kernel(tc, final_features, mid_features, 
 
         def keep_fin(s):
             b, a = divmod(s, TILES)
-            part = late.tile([P, D], F32, name="part")
-            nc.gpsimd.tensor_scalar(
-                out=part[:], in0=fin_sb[b][:, a, :], scalar1=keep[s][:], scalar2=0.0,
-                op0=ALU.mult, op1=ALU.add,
-            )
+            h, j = divmod(s, HALF)
+            if s < ROWS - LAST:
+                part = late.tile([P, D], F32, name="part", bufs=2)
+                nc.gpsimd.tensor_scalar(
+                    out=part[:], in0=fin_sb[b][:, a, :], scalar1=keep[h][:, j : j + 1], scalar2=0.0,
+                    op0=ALU.mult, op1=ALU.add,
+                )
+            else:
+                part = late.tile([P, D], F32, name="part_s", bufs=LAST)
+                nc.scalar.activation(
+                    out=part[:], in_=fin_sb[b][:, a, :], func=FUNC.Copy, scale=keep[h][:, j : j + 1]
+                )
             kept[s] = part
 
         def blend(s):
@@ -320,89 +343,129 @@ def tile_similarityenhancementmodule_t_kernel(tc, final_features, mid_features, 
             if s % 2 == 0:
                 pair = ring.tile([P, 2, D], F32, name="pair")
                 blended[s // 2] = pair
+            to = blended[s // 2][:, s % 2, :]
             nc.vector.scalar_tensor_tensor(
-                out=blended[s // 2][:, s % 2, :], in0=acc[s][:], scalar=gain[h][:, j : j + 1], in1=kept[s][:],
-                op0=ALU.mult, op1=ALU.add,
+                out=to, in0=acc[s][:], scalar=gain[h][:, j : j + 1], in1=kept[s][:], op0=ALU.mult, op1=ALU.add
             )
-            if s % 2 == 1:
+            if s >= ROWS - PAIR:
+                nc.sync.dma_start(out=token_view(out[b])[:, a, :], in_=to)
+            elif s % 2 == 1:
                 nc.sync.dma_start(out=token_view(out[b])[:, a - 1 : a + 1, :], in_=blended[s // 2][:])
 
-        def blends(i):
-            return [i - PV_BEHIND - 1] if i > PV_BEHIND else []
+        def by_vector(s):
+            return s < ROWS and not (False)
 
         def run(stage, index, first, last, *args):
             if first <= index < last:
                 stage(index, *args)
 
-        for half in range(G):
-            u = PACK * half
-            square(u + 3, False)
-            for k in range(3):
-                square(u + k, True)
-            norm(u)
-            regroup_fin(2 * half, False)
-            regroup_fin(2 * half + 1, False)
-        square(TILES, True)
+        for u in (0, 2):
+            square(u, True)
+            square(u + 1, False)
+        first_roots(0)
+        first_norms(0)
         for u in range(PACK):
             scale(u)
             tr_mid(u)
-        quant_fin(0)
-        quant_fin(1)
+        for u in (4, 5, 6):
+            square(u, True)
+        square(7, False)
+        first_roots(PACK)
+        first_norms(PACK)
         for u in range(PACK):
             copy_mid(u, True)
-        square(TILES + 1, True)
         for u in range(PACK, TILES):
             scale(u)
             tr_mid(u)
-        quant_mid(0)
-        quant_mid(1)
-        quant_fin(2)
-        quant_mid(2)
-        quant_fin(3)
-        quant_mid(3)
-        for u in range(PACK, TILES):
-            copy_mid(u, True)
-        for u in range(PACK, TILES):
-            regroup_fin(u, False)
+        for u in range(PACK):
             quant_mid(u)
-        square(TILES + 2, True)
-        square(TILES + 3, True)
-        norm(TILES)
-        square(TILES + 4, True)
-        square(TILES + 5, True)
+        square(TILES, True)
+        regroup_fin(0, "V")
         for u in range(PACK, TILES):
-            quant_fin(u)
-        scale(TILES)
-        tr_mid(TILES)
-        copy_mid(TILES, True)
+            copy_mid(u, True)
+            quant_mid(u)
+        quant_fin(0)
+        for u in range(TILES + 1, TILES + PACK):
+            square(u, True)
+        first_roots(TILES)
+        square(TILES + 4, True)
 
-        for i in range(FIRST, ROWS + PV_BEHIND):
+        def early_engine(u):
+            return "G" if u >= 3 else "V"
+
+        def fin_engine(u):
+            return "G"
+
+        def quant_step(u):
+            return (u - TILES) // 2 + 1 if u < 2 * TILES else u - MID_AHEAD
+
+        def mids(i):
+            return [u for u in range(TILES, ROWS) if quant_step(u) == i]
+
+        def squares(i):
+            return [u for u in range(TILES + 5, ROWS) if i == (u - 16)]
+
+        def early(i):
+            return [u for u in range(1, TILES) if i == (u - 1) // 2 - 1]
+
+        for i in range(FIRST, ROWS + PV_BEHIND + 1):
             done_half = i // HALF if i % HALF == HALF - 1 else -1
-            fin_here = i + FIN_AHEAD
+            ahead = i + FIN_AHEAD + 1
+            norms = i in (1, 4, 8, 12, 16)
             run(tr_e, i - 1, 0, ROWS)
-            run(tr_mid, i + MID_AHEAD - 6, TILES + 1, ROWS)
             run(mask, i + 1, 0, ROWS)
+            for u in mids(i + 1):
+                tr_mid(u)
+            if norms:
+                norm(TILES + PACK if i == 1 else i + 12)
+            if fin_engine(ahead) == "G":
+                run(regroup_fin, ahead, TILES, ROWS, "G")
+            for u in early(i + 1):
+                if early_engine(u) == "G":
+                    regroup_fin(u, "G")
+            run(keep_fin, i - 3, 0, ROWS - LAST)
             run(max_bank, i + 1, 0, ROWS, 0)
             run(max_bank, i + 1, 0, ROWS, 1)
             run(exp_rows, i, 0, ROWS)
             run(pv, i - PV_BEHIND, 0, ROWS)
             run(sim_rows, i + 2, 0, ROWS)
-            run(copy_mid, i + MID_AHEAD - 6, TILES + 1, ROWS, True)
-            run(square, i + MID_AHEAD, TILES + 6, ROWS, True)
+            for u in mids(i + 1):
+                copy_mid(u, True)
+            for u in squares(i):
+                square(u, True)
             run(copy_e, i - 1, 0, ROWS)
-            if (i + 1) % PACK == 0:
-                run(norm, i + MID_AHEAD - 4, TILES + 4, ROWS)
-            for s in blends(i):
-                blend(s)
+            for u in early(i + 1):
+                if early_engine(u) == "S":
+                    regroup_fin(u, "S")
+            if fin_engine(ahead) == "S":
+                run(regroup_fin, ahead, TILES, ROWS, "S")
+            if i == ROWS:
+                for s in range(ROWS - LAST, ROWS):
+                    keep_fin(s)
+            run(blend, i - PV_BEHIND - 1, 0, ROWS)
+            late_e = PV_BEHIND < i and not by_vector(i - PV_BEHIND - 1) or i <= PV_BEHIND
+            if late_e:
+                run(quant_e, i - 2, 0, ROWS)
             run(row_max, i + 1, 0, ROWS)
-            run(scale, i + MID_AHEAD - 5, TILES + 1, ROWS)
+            if i == -1:
+                first_norms(TILES)
+            for u in mids(i + 2):
+                scale(u)
             run(add_sums, done_half, 0, ROWS // HALF)
-            run(quant_e, i - 2, 0, ROWS)
+            for u in early(i):
+                if early_engine(u) == "V":
+                    regroup_fin(u, "V")
+            if fin_engine(ahead) == "V":
+                run(regroup_fin, ahead, TILES, ROWS, "V")
+            if not late_e:
+                run(quant_e, i - 2, 0, ROWS)
             run(invert_sums, done_half, 0, ROWS // HALF)
-            run(quant_mid, i + MID_AHEAD - 7, TILES, ROWS)
-            run(quant_fin, fin_here, TILES, ROWS)
+            for u in mids(i):
+                quant_mid(u)
+            for u in early(i):
+                quant_fin(u)
+            run(quant_fin, i + FIN_AHEAD, TILES, ROWS)
             run(gains, done_half, 0, ROWS // HALF)
-            run(keep_factor, i + 1, 0, ROWS)
-            run(keep_fin, i + 1, 0, ROWS)
-            run(regroup_fin, fin_here + 2, TILES, ROWS, True)
-        blend(ROWS - 1)
+            if i in (0, 3, 7, 11, 15):
+                clamp(TILES + PACK if i == 0 else i + 13)
+            run(keep_factors, i // HALF if i % HALF == 2 else -1, 0, ROWS // HALF)

from contextlib import ExitStack

import concourse.mybir as mybir
from concourse.masks import make_identity

BF16 = mybir.dt.bfloat16
F32 = mybir.dt.float32
U32 = mybir.dt.uint32
U8 = mybir.dt.uint8
FP8X4 = mybir.dt.float8_e4m3fn_x4
ALU = mybir.AluOpType
FUNC = mybir.ActivationFunctionType
AXIS = mybir.AxisListType

B = 4
N = 1024
D = 512
P = 128
PACK = 4
PAIR = 2
K_PASS = P * PACK
TILES = N // P
G = N // K_PASS
BANK = 512
LAST = 3
HALF = PACK
ROWS = B * TILES
EPS = 1e-12

MID_AHEAD = 10
FIN_AHEAD = 5
PV_BEHIND = 3
FIRST = -3

FLOPS = 2 * B * N * N * D * 2


def tile_similarityenhancementmodule_t_kernel(tc, final_features, mid_features, out):
    nc = tc.nc
    with ExitStack() as stack:
        stack.enter_context(tc.manual_schedule())
        const = stack.enter_context(tc.tile_pool(name="const", bufs=1))
        loads = stack.enter_context(tc.tile_pool(name="loads", bufs=B))
        codes = stack.enter_context(tc.tile_pool(name="codes", bufs=3))
        ring = stack.enter_context(tc.tile_pool(name="ring", bufs=4))
        small = stack.enter_context(tc.tile_pool(name="small", bufs=4))
        late = stack.enter_context(tc.tile_pool(name="late", bufs=2 * PV_BEHIND))
        psum = stack.enter_context(tc.psum_pool(name="psum", bufs=2))

        def token_view(dram_batch):
            return dram_batch.rearrange("(a p) d -> p a d", p=P)

        mid_sb = [loads.tile([P, TILES, D], BF16, name="mid_t") for b in range(B)]
        fin_sb = [loads.tile([P, TILES, D], BF16, name="fin_t") for b in range(B)]
        key_sb = [loads.tile([P, G, PACK, D], BF16, name="key_t") for b in range(B)]

        def load_tiles(to, dram, b, first, last):
            nc.sync.dma_start(out=to[b][:, first:last, :], in_=token_view(dram[b])[:, first:last, :])

        def load_keys(b, g):
            view = final_features[b].rearrange("(g p t) d -> p g t d", g=G, p=P, t=PACK)
            nc.sync.dma_start(out=key_sb[b][:, g, :, :], in_=view[:, g, :, :])

        load_tiles(mid_sb, mid_features, 0, 0, 2)
        load_tiles(mid_sb, mid_features, 0, 2, 4)
        load_tiles(mid_sb, mid_features, 0, 4, 8)
        for b in range(B):
            load_keys(b, 0)
            if b + 1 < B:
                load_tiles(mid_sb, mid_features, b + 1, 0, 4)
            load_keys(b, 1)
            load_tiles(fin_sb, final_features, b, 0, 8)
            if b + 1 < B:
                load_tiles(mid_sb, mid_features, b + 1, 4, 8)

        ident_f = const.tile([P, P], F32)
        make_identity(nc, ident_f[:])
        off_diag = const.tile([P, P], F32)
        nc.vector.tensor_scalar(
            out=off_diag[:], in0=ident_f[:], scalar1=-1.0, scalar2=1.0, op0=ALU.mult, op1=ALU.add
        )
        neg_half = const.tile([P, PACK], F32)
        nc.vector.memset(neg_half[:], -0.5)
        sums_ring = [const.tile([P, HALF, 4], F32, name="sums%d" % k) for k in range(3)]
        for k in range(3):
            nc.vector.memset(sums_ring[k][:], 0.0)
        warm = const.tile([P, 1], F32)
        nc.vector.memset(warm[:], 1.0)
        nc.scalar.activation(out=warm[:], in_=warm[:], func=FUNC.Sqrt)

        sumsq, roots, clamped, inv_norm, mid_n, mid_tr, mid_grouped = {}, {}, {}, {}, {}, {}, {}
        mid_codes, mid_scales, fin_codes, fin_scales, fin_grouped = {}, {}, {}, {}, {}
        sim, head, neg_c, sums = {}, {}, {}, {}
        e_row, e_tr, e_grouped, e_codes, e_scales = {}, {}, {}, {}, {}
        row_sum, inv_sum, gain, keep, acc, kept, blended = {}, {}, {}, {}, {}, {}, {}

        def square(u, on_scalar):
            b, a = divmod(u, TILES)
            first = u - u % PACK
            if first not in sumsq:
                total = small.tile([P, PACK], F32, name="total")
                sumsq[first] = total
            squares = ring.tile([P, D], BF16, name="squares")
            tokens = mid_sb[b][:, a, :]
            to = sumsq[first][:, u - first : u - first + 1]
            if on_scalar:
                nc.scalar.activation(out=squares[:], in_=tokens, func=FUNC.Square, accum_out=to)
            else:
                nc.vector.scalar_tensor_tensor(
                    out=squares[:], in0=tokens, scalar=1.0, in1=tokens, op0=ALU.mult, op1=ALU.mult, accum_out=to
                )

        def first_roots(u):
            root = small.tile([P, PACK], F32, name="root")
            nc.scalar.activation(out=root[:], in_=sumsq[u][:], func=FUNC.Sqrt)
            roots[u] = root

        def first_norms(u):
            bounded = small.tile([P, PACK], F32, name="bounded")
            nc.vector.tensor_scalar_max(out=bounded[:], in0=roots[u][:], scalar1=EPS)
            inverse = small.tile([P, PACK], F32, name="inverse")
            nc.vector.reciprocal(out=inverse[:], in_=bounded[:])
            inv_norm[u] = inverse

        def clamp(u):
            bounded = small.tile([P, PACK], F32, name="bounded")
            nc.vector.tensor_scalar_max(out=bounded[:], in0=sumsq[u][:], scalar1=EPS * EPS)
            clamped[u] = bounded

        def norm(u):
            if u not in clamped:
                bounded = small.tile([P, PACK], F32, name="bounded")
                nc.gpsimd.tensor_scalar_max(out=bounded[:], in0=sumsq[u][:], scalar1=EPS * EPS)
                clamped[u] = bounded
            inverse = small.tile([P, PACK], F32, name="inverse")
            nc.gpsimd.tensor_tensor(out=inverse[:], in0=clamped[u][:], in1=neg_half[:], op=ALU.pow)
            inv_norm[u] = inverse

        def scale(u):
            b, a = divmod(u, TILES)
            normed = ring.tile([P, D], BF16, name="normed", align_bytes=64)
            nc.vector.tensor_scalar_mul(out=normed[:], in0=mid_sb[b][:, a, :], scalar1=inv_norm[u - u % PACK][:, u % PACK : u % PACK + 1])
            mid_n[u] = normed

        def tr_mid(u):
            early = u < TILES and u % PACK >= PAIR or TILES <= u < 2 * TILES and u % 2 == 1
            turned = psum.tile([P, PAIR, P], F32, name="mid_turned", tag="pv" if early else "turned")
            words = mid_n[u][:].bitcast(F32)
            for w in range(PAIR):
                nc.tensor.transpose(turned[:, w, :], words[:, w : D // PAIR : PAIR], ident_f[:])
            mid_tr[u] = turned

        def copy_mid(u, on_scalar):
            grouped = ring.tile([P, P, PACK], BF16, name="mid_g", align_bytes=64)
            to = grouped[:].bitcast(F32)
            if on_scalar:
                nc.scalar.copy(out=to, in_=mid_tr[u][:].rearrange("p w m -> p m w"))
            else:
                nc.vector.tensor_copy(out=to, in_=mid_tr[u][:].rearrange("p w m -> p m w"))
            mid_grouped[u] = grouped

        def quant_mid(u):
            b, a = divmod(u, TILES)
            if a == 0:
                words = codes.tile([P, N], U32, name="mid_words", align_bytes=64)
                plane = codes.tile([P, N], U8, name="mid_plane", align_bytes=64)
                mid_codes[b], mid_scales[b] = words, plane
            nc.vector.quantize_mx(
                out=mid_codes[b][:, P * a : P * (a + 1)].bitcast(FP8X4),
                scales=mid_scales[b][:, P * a : P * (a + 1)],
                in_=mid_grouped[u][:].rearrange("p m c -> p (m c)"),
            )

        def regroup_fin(u, engine):
            b, r = divmod(u, TILES)
            g, q = divmod(r, PACK)
            grouped = ring.tile([P, P, PACK], BF16, name="fin_g", tag="fin_" + engine, align_bytes=64, bufs=2)
            rows = key_sb[b][:, g, :, P * q : P * (q + 1)]
            if engine == "S":
                nc.scalar.copy(out=grouped[:], in_=rows.rearrange("p t d -> p d t"))
            elif engine == "G":
                nc.gpsimd.tensor_scalar(
                    out=grouped[:], in0=rows.rearrange("p t d -> p d t"), scalar1=1.0, scalar2=0.0,
                    op0=ALU.mult, op1=ALU.add,
                )
            else:
                nc.vector.tensor_copy(
                    out=grouped[:].rearrange("p (c i) t -> p c t i", i=4),
                    in_=rows.rearrange("p t (c i) -> p c t i", i=4),
                )
            fin_grouped[u] = grouped

        def quant_fin(u):
            b, r = divmod(u, TILES)
            g, q = divmod(r, PACK)
            if r == 0:
                words = codes.tile([P, G, D], U32, name="fin_words", align_bytes=64)
                plane = codes.tile([P, G, D], U8, name="fin_plane", align_bytes=64)
                fin_codes[b], fin_scales[b] = words, plane
            nc.vector.quantize_mx(
                out=fin_codes[b][:, g, P * q : P * (q + 1)].bitcast(FP8X4),
                scales=fin_scales[b][:, g, P * q : P * (q + 1)],
                in_=fin_grouped[u][:].rearrange("p d t -> p (d t)"),
            )

        def sim_rows(s):
            b, a = divmod(s, TILES)
            own = a // PACK
            banks = [psum.tile([P, BANK], F32, name="sim%d" % h) for h in range(2)]

            def product(to, first, last):
                nc.tensor.matmul_mx(
                    out=to,
                    lhsT=mid_codes[b][:, P * a : P * (a + 1)].bitcast(FP8X4),
                    lhsT_scale=mid_scales[b][:, P * a : P * (a + 1)],
                    rhs=mid_codes[b][:, P * first : P * last].bitcast(FP8X4),
                    rhs_scale=mid_scales[b][:, P * first : P * last],
                    start=True,
                    stop=True,
                )

            order = [a] + [k for k in range(PACK * own, PACK * (own + 1)) if k != a]
            for q, k in enumerate(order):
                product(banks[0][:, P * q : P * (q + 1)], k, k + 1)
            other = 1 - own
            product(banks[1][:], PACK * other, PACK * (other + 1))
            sim[s] = banks

        def mask(s):
            h, j = divmod(s, HALF)
            if j == 0:
                minus_c = small.tile([P, HALF], F32, name="minus_c")
                neg_c[h], sums[h] = minus_c, sums_ring[h % 3]
            first = ring.tile([P, P + 2], F32, name="first")
            nc.vector.tensor_tensor(out=first[:, 0:P], in0=sim[s][0][:, 0:P], in1=off_diag[:], op=ALU.mult)
            head[s] = first

        def max_bank(s, h):
            columns = sim[s][h][:, P:BANK] if h == 0 else sim[s][h][:]
            nc.vector.tensor_reduce(out=head[s][:, P + h : P + h + 1], in_=columns, axis=AXIS.X, op=ALU.max)

        def row_max(s):
            h, j = divmod(s, HALF)
            nc.vector.tensor_reduce(out=neg_c[h][:, j : j + 1], in_=head[s][:], axis=AXIS.X, op=ALU.max, negate=True)

        def exp_rows(s):
            a = s % TILES
            own, mine = divmod(a, PACK)
            h, j = divmod(s, HALF)
            e = ring.tile([P, G, PAIR, P, PAIR], BF16, name="e", align_bytes=64)
            parts = [(head[s][:, 0:P], own, mine, mine + 1)]
            if mine > 0:
                parts.append((sim[s][0][:, P : P * (mine + 1)], own, 0, mine))
            if mine < PACK - 1:
                parts.append((sim[s][0][:, P * (mine + 1) : BANK], own, mine + 1, PACK))
            parts.append((sim[s][1][:], 1 - own, 0, PACK))
            share = P // PACK
            for n, (columns, g, first, last) in enumerate(parts):
                nc.scalar.activation(
                    out=e[:, g, :, share * first : share * last, :],
                    in_=columns.rearrange("q (p w i) -> q w p i", w=PAIR, i=PAIR),
                    func=FUNC.Exp, bias=neg_c[h][:, j : j + 1], accum_out=sums[h][:, j, n : n + 1],
                )
            e_row[s] = e

        def tr_e(s):
            turned = psum.tile([P, G, PAIR, P], F32, name="e_turned", tag="turned")
            for g in range(G):
                for w in range(PAIR):
                    words = e_row[s][:, g, w, :, :].rearrange("q p i -> q (p i)").bitcast(F32)
                    nc.tensor.transpose(turned[:, g, w, :], words, ident_f[:])
            e_tr[s] = turned

        def copy_e(s):
            grouped = ring.tile([P, G, P, PACK], BF16, name="e_g", align_bytes=64)
            nc.scalar.copy(out=grouped[:].bitcast(F32), in_=e_tr[s][:].rearrange("p g w m -> p g m w"))
            e_grouped[s] = grouped

        def quant_e(s):
            words = late.tile([P, G * P], U32, name="e_words", align_bytes=64)
            plane = late.tile([P, G * P], U8, name="e_plane", align_bytes=64)
            nc.vector.quantize_mx(
                out=words[:].bitcast(FP8X4), scales=plane[:], in_=e_grouped[s][:].rearrange("p g m t -> p (g m t)")
            )
            e_codes[s], e_scales[s] = words, plane

        def add_sums(h):
            total = small.tile([P, HALF], F32, name="row_total")
            nc.vector.tensor_reduce(out=total[:], in_=sums[h][:], axis=AXIS.X, op=ALU.add)
            row_sum[h] = total

        def invert_sums(h):
            inverse = small.tile([P, HALF], F32, name="row_inverse")
            nc.vector.reciprocal(out=inverse[:], in_=row_sum[h][:])
            inv_sum[h] = inverse

        def gains(h):
            c_over_sum = small.tile([P, HALF], F32)
            nc.vector.scalar_tensor_tensor(
                out=c_over_sum[:], in0=neg_c[h][:], scalar=-1.0, in1=inv_sum[h][:], op0=ALU.mult, op1=ALU.mult
            )
            gain[h] = c_over_sum

        def keep_factors(h):
            one_minus_c = small.tile([P, HALF], F32)
            nc.vector.tensor_scalar_add(out=one_minus_c[:], in0=neg_c[h][:], scalar1=1.0)
            keep[h] = one_minus_c

        def pv(s):
            b = s // TILES
            total = psum.tile([P, D], F32, name="pv_total", tag="pv")
            for g in range(G):
                nc.tensor.matmul_mx(
                    out=total[:],
                    lhsT=e_codes[s][:, P * g : P * (g + 1)].bitcast(FP8X4),
                    lhsT_scale=e_scales[s][:, P * g : P * (g + 1)],
                    rhs=fin_codes[b][:, g, :].bitcast(FP8X4),
                    rhs_scale=fin_scales[b][:, g, :],
                    start=(g == 0),
                    stop=(g == G - 1),
                )
            acc[s] = total

        def keep_fin(s):
            b, a = divmod(s, TILES)
            h, j = divmod(s, HALF)
            if s < ROWS - LAST:
                part = late.tile([P, D], F32, name="part", bufs=2)
                nc.gpsimd.tensor_scalar(
                    out=part[:], in0=fin_sb[b][:, a, :], scalar1=keep[h][:, j : j + 1], scalar2=0.0,
                    op0=ALU.mult, op1=ALU.add,
                )
            else:
                part = late.tile([P, D], F32, name="part_s", bufs=LAST)
                nc.scalar.activation(
                    out=part[:], in_=fin_sb[b][:, a, :], func=FUNC.Copy, scale=keep[h][:, j : j + 1]
                )
            kept[s] = part

        def blend(s):
            b, a = divmod(s, TILES)
            h, j = divmod(s, HALF)
            if s % 2 == 0:
                pair = ring.tile([P, 2, D], F32, name="pair")
                blended[s // 2] = pair
            to = blended[s // 2][:, s % 2, :]
            nc.vector.scalar_tensor_tensor(
                out=to, in0=acc[s][:], scalar=gain[h][:, j : j + 1], in1=kept[s][:], op0=ALU.mult, op1=ALU.add
            )
            if s >= ROWS - PAIR:
                nc.sync.dma_start(out=token_view(out[b])[:, a, :], in_=to)
            elif s % 2 == 1:
                nc.sync.dma_start(out=token_view(out[b])[:, a - 1 : a + 1, :], in_=blended[s // 2][:])

        def by_vector(s):
            return s < ROWS and not (False)

        def run(stage, index, first, last, *args):
            if first <= index < last:
                stage(index, *args)

        for u in (0, 2):
            square(u, True)
            square(u + 1, False)
        first_roots(0)
        first_norms(0)
        for u in range(PACK):
            scale(u)
            tr_mid(u)
        for u in (4, 5, 6):
            square(u, True)
        square(7, False)
        first_roots(PACK)
        first_norms(PACK)
        for u in range(PACK):
            copy_mid(u, True)
        for u in range(PACK, TILES):
            scale(u)
            tr_mid(u)
        for u in range(PACK):
            quant_mid(u)
        square(TILES, True)
        regroup_fin(0, "V")
        for u in range(PACK, TILES):
            copy_mid(u, True)
            quant_mid(u)
        quant_fin(0)
        for u in range(TILES + 1, TILES + PACK):
            square(u, True)
        first_roots(TILES)
        square(TILES + 4, True)

        def early_engine(u):
            return "G" if u >= 3 else "V"

        def fin_engine(u):
            return "G"

        def quant_step(u):
            return (u - TILES) // 2 + 1 if u < 2 * TILES else u - MID_AHEAD

        def mids(i):
            return [u for u in range(TILES, ROWS) if quant_step(u) == i]

        def squares(i):
            return [u for u in range(TILES + 5, ROWS) if i == (u - 16)]

        def early(i):
            return [u for u in range(1, TILES) if i == (u - 1) // 2 - 1]

        for i in range(FIRST, ROWS + PV_BEHIND + 1):
            done_half = i // HALF if i % HALF == HALF - 1 else -1
            ahead = i + FIN_AHEAD + 1
            norms = i in (1, 4, 8, 12, 16)
            run(tr_e, i - 1, 0, ROWS)
            run(mask, i + 1, 0, ROWS)
            for u in mids(i + 1):
                tr_mid(u)
            if norms:
                norm(TILES + PACK if i == 1 else i + 12)
            if fin_engine(ahead) == "G":
                run(regroup_fin, ahead, TILES, ROWS, "G")
            for u in early(i + 1):
                if early_engine(u) == "G":
                    regroup_fin(u, "G")
            run(keep_fin, i - 3, 0, ROWS - LAST)
            run(max_bank, i + 1, 0, ROWS, 0)
            run(max_bank, i + 1, 0, ROWS, 1)
            run(exp_rows, i, 0, ROWS)
            run(pv, i - PV_BEHIND, 0, ROWS)
            run(sim_rows, i + 2, 0, ROWS)
            for u in mids(i + 1):
                copy_mid(u, True)
            for u in squares(i):
                square(u, True)
            run(copy_e, i - 1, 0, ROWS)
            for u in early(i + 1):
                if early_engine(u) == "S":
                    regroup_fin(u, "S")
            if fin_engine(ahead) == "S":
                run(regroup_fin, ahead, TILES, ROWS, "S")
            if i == ROWS:
                for s in range(ROWS - LAST, ROWS):
                    keep_fin(s)
            run(blend, i - PV_BEHIND - 1, 0, ROWS)
            late_e = PV_BEHIND < i and not by_vector(i - PV_BEHIND - 1) or i <= PV_BEHIND
            if late_e:
                run(quant_e, i - 2, 0, ROWS)
            run(row_max, i + 1, 0, ROWS)
            if i == -1:
                first_norms(TILES)
            for u in mids(i + 2):
                scale(u)
            run(add_sums, done_half, 0, ROWS // HALF)
            for u in early(i):
                if early_engine(u) == "V":
                    regroup_fin(u, "V")
            if fin_engine(ahead) == "V":
                run(regroup_fin, ahead, TILES, ROWS, "V")
            if not late_e:
                run(quant_e, i - 2, 0, ROWS)
            run(invert_sums, done_half, 0, ROWS // HALF)
            for u in mids(i):
                quant_mid(u)
            for u in early(i):
                quant_fin(u)
            run(quant_fin, i + FIN_AHEAD, TILES, ROWS)
            run(gains, done_half, 0, ROWS // HALF)
            if i in (0, 3, 7, 11, 15):
                clamp(TILES + PACK if i == 0 else i + 13)
            run(keep_factors, i // HALF if i % HALF == 2 else -1, 0, ROWS // HALF)
